import numpy as np
import ml_dtypes


def mxq(x, axis, fmt="e4m3"):
    dtype, down = {"e4m3": (ml_dtypes.float8_e4m3fn, 7), "e5m2": (ml_dtypes.float8_e5m2, 14)}[fmt]
    v = np.moveaxis(np.asarray(x, np.float32).astype(ml_dtypes.bfloat16).astype(np.float64), axis, -1)
    blocks = v.reshape(v.shape[:-1] + (-1, 32))
    amax = np.abs(blocks).max(-1, keepdims=True)
    byte = np.maximum(np.where(amax > 0, np.frexp(amax)[1] - 1 + 127, 0) - down, 1)
    scale = np.exp2(byte - 127.0)
    codes = (blocks / scale).astype(np.float32).astype(dtype).astype(np.float64)
    return np.moveaxis((codes * scale).reshape(v.shape), -1, axis)


WIDE = False


def mx_kscale(k):
    if not WIDE:
        return np.ones(k)
    levels = np.array([10, -10, 5, -5, 0])
    if k % 512:
        return np.exp2(np.random.permutation(np.resize(levels, k // 32))).repeat(32)
    a = np.empty((k // 512, 16))
    for p in range(k // 512):
        a[p, :8] = np.random.permutation(np.resize(levels, 8))
        for g in range(8):
            far = levels[np.abs(levels - a[p, g]) >= 10]
            a[p, g + 8] = far[np.random.randint(len(far))]
    return np.exp2(a.ravel()).repeat(32)


BF16 = ml_dtypes.bfloat16


def bf(x):
    return np.asarray(x, np.float32).astype(BF16)


def f64(x):
    return np.asarray(x).astype(np.float64)


B, P, D = 4096, 2, 512
IN = P * D


def sigmoid(v):
    return 1.0 / (1.0 + np.exp(-v))


def setup_inputs():
    s = mx_kscale(D)
    sf = np.tile(s, P)
    return {"x": bf(np.random.standard_normal((B, IN)) * sf),
            "weights": bf(np.random.standard_normal((P, D, D)) / np.sqrt(D) / s[None, :, None] * s[None, None, :]),
            "bias": bf(np.random.standard_normal(IN) * 0.3 * sf),
            "gain": bf(1.3 + 0.1 * np.random.standard_normal(1)),
            "norm_bias": bf((0.3 + 0.05 * np.random.standard_normal(1)) * s.min()),
            "gamma": bf(0.5 + 0.3 * np.random.standard_normal(IN)),
            "beta": bf(np.random.standard_normal(IN) / sf)}


def reference(x, weights, bias, gain, norm_bias, gamma, beta):
    x, gamma = f64(x), f64(gamma)
    x_norm = x * f64(gain) + f64(norm_bias)
    xp = x_norm.reshape(B, P, D)
    yp = mxq(xp, 2, "e4m3").transpose(1, 0, 2) @ mxq(f64(weights), 1, "e4m3")
    y = yp.transpose(1, 0, 2).reshape(B, IN) + f64(bias)
    mult = gamma + sigmoid(f64(beta) * y) * (1.0 - gamma)
    o = mult * y
    return o + x

@@ -1,0 +1,256 @@
+from contextlib import ExitStack
+
+import concourse.mybir as mybir
+from concourse.masks import make_identity
+
+F32 = mybir.dt.float32
+BF16 = mybir.dt.bfloat16
+U32 = mybir.dt.uint32
+U8 = mybir.dt.uint8
+FP8X4 = mybir.dt.float8_e4m3fn_x4
+ACT = mybir.ActivationFunctionType
+ALU = mybir.AluOpType
+
+P = 128
+B = 4096
+PARTS = 2
+D = 512
+IN = PARTS * D
+ROWS = 512
+JT = ROWS // P
+NBLK = B // ROWS
+NU = NBLK * PARTS
+CC = D // P
+FLOPS = 2 * B * D * D * PARTS
+MANUAL = False
+
+
+def tile_better_transformer_t_kernel(tc, x, weights, bias, gain, norm_bias, gamma, beta, out):
+    nc = tc.nc
+    with ExitStack() as ctx:
+        const = ctx.enter_context(tc.tile_pool(name="const", bufs=1))
+        xin = ctx.enter_context(tc.tile_pool(name="xin", bufs=NBLK))
+        work = ctx.enter_context(tc.tile_pool(name="work", bufs=3))
+        psum = ctx.enter_context(tc.psum_pool(name="psum", bufs=2))
+
+        ident = const.tile([P, P], F32, name="ident")
+        make_identity(nc, ident[:])
+
+        gain_bf = const.tile([P, 1], BF16, name="gain_bf")
+        nb_bf = const.tile([P, 1], BF16, name="nb_bf")
+        nc.scalar.dma_start(out=gain_bf[:], in_=gain.partition_broadcast(P))
+        nc.scalar.dma_start(out=nb_bf[:], in_=norm_bias.partition_broadcast(P))
+        prm_bf = const.tile([P, P], BF16, name="prm_bf")
+        nc.vector.memset(prm_bf[:], 0.0)
+        nc.scalar.dma_start(out=prm_bf[0:8, :], in_=bias.rearrange("(r c) -> r c", c=P))
+        nc.scalar.dma_start(out=prm_bf[8:16, :], in_=gamma.rearrange("(r c) -> r c", c=P))
+        nc.scalar.dma_start(out=prm_bf[16:24, :], in_=beta.rearrange("(r c) -> r c", c=P))
+        warm = const.tile([P, 1], F32, name="warm")
+        nc.vector.memset(warm[:], 0.0)
+        nc.scalar.activation(out=warm[:], in_=warm[:], func=ACT.Sigmoid)
+
+        x_sb = []
+        for i in range(NBLK):
+            xt_i = xin.tile([P, JT * IN], BF16, name="x_sb")
+            x_sb.append(xt_i)
+        wraw = const.tile([P, PARTS * 4 * D], BF16, name="wraw")
+
+        def load_x(i):
+            nc.sync.dma_start(
+                out=x_sb[i][:],
+                in_=x[i * ROWS : (i + 1) * ROWS, :].rearrange("(p j) k -> p (j k)", j=JT),
+            )
+
+        for g in range(PARTS):
+            nc.sync.dma_start(
+                out=x_sb[0][:].rearrange("p (j k) -> p j k", j=JT)[:, :, g * D : (g + 1) * D],
+                in_=x[0:ROWS, g * D : (g + 1) * D].rearrange("(p j) k -> p j k", j=JT),
+            )
+            nc.sync.dma_start(
+                out=wraw[:, g * 4 * D : (g + 1) * 4 * D],
+                in_=weights[g : g + 1, :, :].rearrange("o (p t) c -> p (o t c)", t=4),
+            )
+        for i in range(1, NBLK):
+            load_x(i)
+
+        gain_f = const.tile([P, 1], F32, name="gain_f")
+        nb_f = const.tile([P, 1], F32, name="nb_f")
+        nc.vector.tensor_copy(out=gain_f[:], in_=gain_bf[:])
+        nc.vector.tensor_copy(out=nb_f[:], in_=nb_bf[:])
+
+        def prep():
+            prm_f = const.tile([P, P], F32, name="prm_f")
+            nc.vector.tensor_copy(out=prm_f[:], in_=prm_bf[:])
+            prm_ps = psum.tile([P, 512], F32, name="prm_ps", tag="xt")
+            nc.tensor.transpose(prm_ps[:, 0:P], prm_f[:], ident[:])
+            prm = const.tile([P, 32], F32, name="prm")
+            nc.vector.tensor_copy(out=prm[:], in_=prm_ps[:, 0:32])
+            bb = const.tile([P, 8], F32, name="bb")
+            nc.vector.tensor_tensor(out=bb[:], in0=prm[:, 16:24], in1=prm[:, 0:8], op=ALU.mult)
+            dd = const.tile([P, 8], F32, name="dd")
+            nc.vector.tensor_scalar(out=dd[:], in0=prm[:, 8:16], scalar1=-1.0, scalar2=1.0, op0=ALU.mult, op1=ALU.add)
+
+            wgrp = const.tile([P, PARTS * 4 * D], BF16, name="wgrp", align_bytes=64)
+            wc = const.tile([P, PARTS * D], U32, name="wc", align_bytes=64)
+            ws = const.tile([P, PARTS * D], U8, name="ws", align_bytes=64)
+            for g in range(PARTS):
+                dst = wgrp[:, g * 4 * D : (g + 1) * 4 * D].rearrange("p (c t) -> p c t", t=4)
+                src = wraw[:, g * 4 * D : (g + 1) * 4 * D].rearrange("p (t c) -> p c t", t=4)
+                if g == 0:
+                    nc.vector.tensor_copy(out=dst, in_=src)
+                else:
+                    nc.scalar.copy(out=dst, in_=src)
+            for g in range(PARTS):
+                nc.vector.quantize_mx(
+                    out=wc[:, g * D : (g + 1) * D].bitcast(FP8X4),
+                    scales=ws[:, g * D : (g + 1) * D],
+                    in_=wgrp[:, g * 4 * D : (g + 1) * 4 * D],
+                )
+
+            cst["prm"] = prm
+            cst["bb"] = bb
+            cst["dd"] = dd
+            cst["wc"] = wc
+            cst["ws"] = ws
+
+        cst = {}
+        xg = {}
+        xc = {}
+        xs = {}
+        acc = {}
+        mm = {}
+        op = {}
+        ob = {}
+        ots = {}
+
+        def stage_a(h, jp):
+            i, g = divmod(h, PARTS)
+            xw = x_sb[i][:].bitcast(F32)
+            if jp == 0:
+                xg[h] = work.tile([P, 4 * ROWS], BF16, name="xg", align_bytes=64)
+            if True:
+                xt = psum.tile([P, 512], F32, name="xt", tag="xt")
+                for u in range(2):
+                    for jj in range(2):
+                        j = 2 * jp + jj
+                        col = j * (IN // 2) + g * (D // 2)
+                        nc.tensor.transpose(
+                            xt[:, u * 256 + jj * P : u * 256 + (jj + 1) * P], xw[:, col + u : col + D // 2 : 2], ident[:]
+                        )
+                xg_dst = xg[h][:, jp * 1024 : (jp + 1) * 1024].rearrange("p (n u e) -> p n u e", u=2, e=2)
+                xt_src = xt[:].bitcast(BF16).rearrange("p (u n e) -> p n u e", u=2, e=2)
+                if h < 2 and jp == 1:
+                    nc.vector.tensor_scalar(
+                        out=xg_dst, in0=xt_src, scalar1=gain_f[:, 0:1], scalar2=nb_f[:, 0:1], op0=ALU.mult, op1=ALU.add
+                    )
+                else:
+                    nc.scalar.activation(
+                        out=xg_dst, in_=xt_src, func=ACT.Identity, scale=gain_f[:, 0:1], bias=nb_f[:, 0:1]
+                    )
+
+        def stage_q(h):
+            xc[h] = work.tile([P, ROWS], U32, name="xc", align_bytes=64)
+            xs[h] = work.tile([P, ROWS], U8, name="xs", align_bytes=64)
+            nc.vector.quantize_mx(out=xc[h][:].bitcast(FP8X4), scales=xs[h][:], in_=xg[h][:])
+
+        def stage_mx(h, k):
+            g = h % PARTS
+            q = g * CC + k
+            a = psum.tile([P, ROWS], F32, name="acc", tag="acc", bufs=4)
+            acc[(h, k)] = a
+            nc.tensor.matmul_mx(
+                out=a[:],
+                lhsT=cst["wc"][:, q * P : (q + 1) * P].bitcast(FP8X4),
+                lhsT_scale=cst["ws"][:, q * P : (q + 1) * P],
+                rhs=xc[h][:].bitcast(FP8X4),
+                rhs_scale=xs[h][:],
+                start=True,
+                stop=True,
+            )
+            s = work.tile([P, ROWS], F32, name="sg", bufs=4)
+            nc.scalar.activation(
+                out=s[:], in_=a[:], func=ACT.Sigmoid, scale=cst["prm"][:, 16 + q : 17 + q], bias=cst["bb"][:, q : q + 1]
+            )
+            m = work.tile([P, ROWS], F32, name="mm", bufs=8)
+            mm[(h, k)] = m
+            nc.gpsimd.tensor_scalar(
+                out=m[:], in0=s[:], scalar1=cst["dd"][:, q : q + 1], scalar2=cst["prm"][:, 8 + q : 9 + q], op0=ALU.mult, op1=ALU.add
+            )
+
+        def stage_prod(h, k):
+            q = (h % PARTS) * CC + k
+            if k == 0:
+                op[h] = work.tile([P, CC * ROWS], F32, name="op")
+            nc.vector.scalar_tensor_tensor(
+                out=op[h][:, k * ROWS : (k + 1) * ROWS],
+                in0=acc[(h, k)][:],
+                scalar=cst["prm"][:, q : q + 1],
+                in1=mm[(h, k)][:],
+                op0=ALU.add,
+                op1=ALU.mult,
+            )
+
+        def stage_back(h, j):
+            ot = psum.tile([P, D], F32, name="ot", tag="ot")
+            ots[(h, j)] = ot
+            for k in range(CC):
+                nc.tensor.transpose(
+                    ot[:, k * P : (k + 1) * P], op[h][:, k * ROWS + j * P : k * ROWS + (j + 1) * P], ident[:]
+                )
+
+        def stage_res(h, j):
+            i, g = divmod(h, PARTS)
+            if j == 0:
+                ob[h] = work.tile([P, JT * D], F32, name="ob", bufs=4)
+            if h % 2 == 1 and j == 1 and h < NU - 1:
+                nc.scalar.copy(out=ob[h][:, j * D : (j + 1) * D], in_=ots[(h, j)][:])
+                nc.gpsimd.tensor_tensor(
+                    out=ob[h][:, j * D : (j + 1) * D],
+                    in0=ob[h][:, j * D : (j + 1) * D],
+                    in1=x_sb[i][:, j * IN + g * D : j * IN + (g + 1) * D],
+                    op=ALU.add,
+                )
+            else:
+                nc.vector.tensor_tensor(
+                    out=ob[h][:, j * D : (j + 1) * D],
+                    in0=ots[(h, j)][:],
+                    in1=x_sb[i][:, j * IN + g * D : j * IN + (g + 1) * D],
+                    op=ALU.add,
+                )
+            dst = out[i * ROWS : (i + 1) * ROWS, g * D : (g + 1) * D].rearrange("(p j) c -> p j c", j=JT)
+            src = ob[h][:].rearrange("p (j c) -> p j c", j=JT)
+            if h == NU - 1:
+                nc.sync.dma_start(out=dst[:, j : j + 1, :], in_=src[:, j : j + 1, :])
+            elif j == JT - 1:
+                nc.sync.dma_start(out=dst, in_=src)
+
+        def ok(h):
+            return 0 <= h < NU
+
+        def main_loop():
+            for h in range(-3, NU + 1):
+                if ok(h + 2):
+                    stage_q(h + 2)
+                for k in range(CC):
+                    if ok(h):
+                        stage_prod(h, k)
+                    if ok(h + 1):
+                        stage_mx(h + 1, k)
+                    if ok(h - 1):
+                        stage_res(h - 1, k)
+                    if k < 2:
+                        if ok(h - 1):
+                            stage_back(h - 1, k + 2)
+                        if ok(h + 3):
+                            stage_a(h + 3, k)
+                if ok(h):
+                    stage_back(h, 0)
+                    stage_back(h, 1)
+                if h == -3:
+                    prep()
+
+        if MANUAL:
+            with tc.manual_schedule():
+                main_loop()
+        else:
+            main_loop()

@@ -30,6 +30,7 @@ def tile_better_transformer_t_kernel(tc, x, weights, bias, gain, norm_bias, gamm
     with ExitStack() as ctx:
         const = ctx.enter_context(tc.tile_pool(name="const", bufs=1))
         xin = ctx.enter_context(tc.tile_pool(name="xin", bufs=NBLK))
+        xnp = ctx.enter_context(tc.tile_pool(name="xnp", bufs=3))
         work = ctx.enter_context(tc.tile_pool(name="work", bufs=3))
         psum = ctx.enter_context(tc.psum_pool(name="psum", bufs=2))
 
@@ -114,6 +115,7 @@ def tile_better_transformer_t_kernel(tc, x, weights, bias, gain, norm_bias, gamm
             cst["ws"] = ws
 
         cst = {}
+        xn = {}
         xg = {}
         xc = {}
         xs = {}
@@ -123,9 +125,24 @@ def tile_better_transformer_t_kernel(tc, x, weights, bias, gain, norm_bias, gamm
         ob = {}
         ots = {}
 
+        def norm_x(i, u, g=None):
+            if i not in xn:
+                xn[i] = xnp.tile([P, JT * IN], BF16, name="xn")
+            dst = xn[i][:].rearrange("p (u j g w e) -> p u j g w e", u=2, j=JT, g=PARTS, e=2)[:, u]
+            src = x_sb[i][:].rearrange("p (j g w u e) -> p u j g w e", u=2, j=JT, g=PARTS, e=2)[:, u]
+            if g is None:
+                dst = xn[i][:].rearrange("p (u a e) -> p u a e", u=2, e=2)[:, u]
+                src = x_sb[i][:].rearrange("p (a u e) -> p u a e", u=2, e=2)[:, u]
+            else:
+                dst = dst[:, :, g]
+                src = src[:, :, g]
+            nc.vector.tensor_scalar(
+                out=dst, in0=src, scalar1=gain_f[:, 0:1], scalar2=nb_f[:, 0:1], op0=ALU.mult, op1=ALU.add
+            )
+
         def stage_a(h, jp):
             i, g = divmod(h, PARTS)
-            xw = x_sb[i][:].bitcast(F32)
+            xw = xn[i][:].bitcast(F32)
             if jp == 0:
                 xg[h] = work.tile([P, 4 * ROWS], BF16, name="xg", align_bytes=64)
             if True:
@@ -133,20 +150,14 @@ def tile_better_transformer_t_kernel(tc, x, weights, bias, gain, norm_bias, gamm
                 for u in range(2):
                     for jj in range(2):
                         j = 2 * jp + jj
-                        col = j * (IN // 2) + g * (D // 2)
+                        col = u * (JT * IN // 4) + (j * PARTS + g) * P
                         nc.tensor.transpose(
-                            xt[:, u * 256 + jj * P : u * 256 + (jj + 1) * P], xw[:, col + u : col + D // 2 : 2], ident[:]
+                            xt[:, u * 256 + jj * P : u * 256 + (jj + 1) * P], xw[:, col : col + P], ident[:]
                         )
-                xg_dst = xg[h][:, jp * 1024 : (jp + 1) * 1024].rearrange("p (n u e) -> p n u e", u=2, e=2)
-                xt_src = xt[:].bitcast(BF16).rearrange("p (u n e) -> p n u e", u=2, e=2)
-                if h < 2 and jp == 1:
-                    nc.vector.tensor_scalar(
-                        out=xg_dst, in0=xt_src, scalar1=gain_f[:, 0:1], scalar2=nb_f[:, 0:1], op0=ALU.mult, op1=ALU.add
-                    )
-                else:
-                    nc.scalar.activation(
-                        out=xg_dst, in_=xt_src, func=ACT.Identity, scale=gain_f[:, 0:1], bias=nb_f[:, 0:1]
-                    )
+                nc.scalar.copy(
+                    out=xg[h][:, jp * 1024 : (jp + 1) * 1024].bitcast(F32).rearrange("p (n u) -> p n u", u=2),
+                    in_=xt[:].rearrange("p (u n) -> p n u", u=2),
+                )
 
         def stage_q(h):
             xc[h] = work.tile([P, ROWS], U32, name="xc", align_bytes=64)
@@ -229,6 +240,10 @@ def tile_better_transformer_t_kernel(tc, x, weights, bias, gain, norm_bias, gamm
 
         def main_loop():
             for h in range(-3, NU + 1):
+                if h == -3:
+                    for g in range(PARTS):
+                        for u in range(2):
+                            norm_x(0, u, g)
                 if ok(h + 2):
                     stage_q(h + 2)
                 for k in range(CC):
@@ -238,6 +253,8 @@ def tile_better_transformer_t_kernel(tc, x, weights, bias, gain, norm_bias, gamm
                         stage_mx(h + 1, k)
                     if ok(h - 1):
                         stage_res(h - 1, k)
+                    if k == 2 and 2 <= h + 5 < NU:
+                        norm_x((h + 5) // 2, (h + 5) % 2)
                     if k < 2:
                         if ok(h - 1):
                             stage_back(h - 1, k + 2)

@@ -36,6 +36,8 @@ def tile_better_transformer_t_kernel(tc, x, weights, bias, gain, norm_bias, gamm
 
         ident = const.tile([P, P], F32, name="ident")
         make_identity(nc, ident[:])
+        ident_bf = const.tile([P, P], BF16, name="ident_bf")
+        nc.vector.tensor_copy(out=ident_bf[:], in_=ident[:])
 
         gain_bf = const.tile([P, 1], BF16, name="gain_bf")
         nb_bf = const.tile([P, 1], BF16, name="nb_bf")
@@ -201,26 +203,33 @@ def tile_better_transformer_t_kernel(tc, x, weights, bias, gain, norm_bias, gamm
                 op1=ALU.mult,
             )
 
+        def on_pe(h, j):
+            return j == 1 or (j == 3 and h % 2 == 1)
+
         def stage_back(h, j):
+            i, g = divmod(h, PARTS)
             ot = psum.tile([P, D], F32, name="ot", tag="ot")
             ots[(h, j)] = ot
+            if on_pe(h, j):
+                nc.tensor.matmul(
+                    ot[:], lhsT=ident_bf[:], rhs=x_sb[i][:, j * IN + g * D : j * IN + (g + 1) * D], start=True, stop=False
+                )
             for k in range(CC):
-                nc.tensor.transpose(
-                    ot[:, k * P : (k + 1) * P], op[h][:, k * ROWS + j * P : k * ROWS + (j + 1) * P], ident[:]
+                nc.tensor.matmul(
+                    ot[:, k * P : (k + 1) * P],
+                    lhsT=op[h][:, k * ROWS + j * P : k * ROWS + (j + 1) * P],
+                    rhs=ident[:],
+                    is_transpose=True,
+                    start=not on_pe(h, j),
+                    stop=not on_pe(h, j) or k == CC - 1,
                 )
 
         def stage_res(h, j):
             i, g = divmod(h, PARTS)
             if j == 0:
                 ob[h] = work.tile([P, JT * D], F32, name="ob", bufs=4)
-            if h % 2 == 1 and j == 1 and h < NU - 1:
+            if on_pe(h, j):
                 nc.scalar.copy(out=ob[h][:, j * D : (j + 1) * D], in_=ots[(h, j)][:])
-                nc.gpsimd.tensor_tensor(
-                    out=ob[h][:, j * D : (j + 1) * D],
-                    in0=ob[h][:, j * D : (j + 1) * D],
-                    in1=x_sb[i][:, j * IN + g * D : j * IN + (g + 1) * D],
-                    op=ALU.add,
-                )
             else:
                 nc.vector.tensor_tensor(
                     out=ob[h][:, j * D : (j + 1) * D],

@@ -21,27 +21,22 @@ JT = ROWS // P
 NBLK = B // ROWS
 NU = NBLK * PARTS
 CC = D // P
+HC = D // 2
 FLOPS = 2 * B * D * D * PARTS
-MANUAL = False
 
 
 def tile_better_transformer_t_kernel(tc, x, weights, bias, gain, norm_bias, gamma, beta, out):
     nc = tc.nc
     with ExitStack() as ctx:
         const = ctx.enter_context(tc.tile_pool(name="const", bufs=1))
-        xin = ctx.enter_context(tc.tile_pool(name="xin", bufs=NBLK))
+        xin = ctx.enter_context(tc.tile_pool(name="xin", bufs=NBLK - 1))
         xnp = ctx.enter_context(tc.tile_pool(name="xnp", bufs=3))
         work = ctx.enter_context(tc.tile_pool(name="work", bufs=3))
         psum = ctx.enter_context(tc.psum_pool(name="psum", bufs=2))
 
-        ident = const.tile([P, P], F32, name="ident")
-        make_identity(nc, ident[:])
-        ident_bf = const.tile([P, P], BF16, name="ident_bf")
-        nc.vector.tensor_copy(out=ident_bf[:], in_=ident[:])
-
         gain_bf = const.tile([P, 1], BF16, name="gain_bf")
         nb_bf = const.tile([P, 1], BF16, name="nb_bf")
-        nc.scalar.dma_start(out=gain_bf[:], in_=gain.partition_broadcast(P))
+        nc.sync.dma_start(out=gain_bf[:], in_=gain.partition_broadcast(P))
         nc.scalar.dma_start(out=nb_bf[:], in_=norm_bias.partition_broadcast(P))
         prm_bf = const.tile([P, P], BF16, name="prm_bf")
         nc.vector.memset(prm_bf[:], 0.0)
@@ -52,21 +47,18 @@ def tile_better_transformer_t_kernel(tc, x, weights, bias, gain, norm_bias, gamm
         nc.vector.memset(warm[:], 0.0)
         nc.scalar.activation(out=warm[:], in_=warm[:], func=ACT.Sigmoid)
 
-        x_sb = []
-        for i in range(NBLK):
+        x0 = []
+        for g in range(PARTS):
+            x0_g = const.tile([P, JT * D], BF16, name="x0_%d" % g)
+            x0.append(x0_g)
+        x_sb = [None]
+        for i in range(1, NBLK):
             xt_i = xin.tile([P, JT * IN], BF16, name="x_sb")
             x_sb.append(xt_i)
         wraw = const.tile([P, PARTS * 4 * D], BF16, name="wraw")
-
-        def load_x(i):
-            nc.sync.dma_start(
-                out=x_sb[i][:],
-                in_=x[i * ROWS : (i + 1) * ROWS, :].rearrange("(p j) k -> p (j k)", j=JT),
-            )
-
         for g in range(PARTS):
             nc.sync.dma_start(
-                out=x_sb[0][:].rearrange("p (j k) -> p j k", j=JT)[:, :, g * D : (g + 1) * D],
+                out=x0[g][:].rearrange("p (j k) -> p j k", j=JT),
                 in_=x[0:ROWS, g * D : (g + 1) * D].rearrange("(p j) k -> p j k", j=JT),
             )
             nc.sync.dma_start(
@@ -74,49 +66,23 @@ def tile_better_transformer_t_kernel(tc, x, weights, bias, gain, norm_bias, gamm
                 in_=weights[g : g + 1, :, :].rearrange("o (p t) c -> p (o t c)", t=4),
             )
         for i in range(1, NBLK):
-            load_x(i)
+            nc.sync.dma_start(
+                out=x_sb[i][:],
+                in_=x[i * ROWS : (i + 1) * ROWS, :].rearrange("(p j) k -> p (j k)", j=JT),
+            )
 
-        gain_f = const.tile([P, 1], F32, name="gain_f")
-        nb_f = const.tile([P, 1], F32, name="nb_f")
-        nc.vector.tensor_copy(out=gain_f[:], in_=gain_bf[:])
-        nc.vector.tensor_copy(out=nb_f[:], in_=nb_bf[:])
+        ident = const.tile([P, P], F32, name="ident")
+        make_identity(nc, ident[:])
+        ident_bf = const.tile([P, P], BF16, name="ident_bf")
+        nc.vector.tensor_copy(out=ident_bf[:], in_=ident[:])
 
-        def prep():
-            prm_f = const.tile([P, P], F32, name="prm_f")
-            nc.vector.tensor_copy(out=prm_f[:], in_=prm_bf[:])
-            prm_ps = psum.tile([P, 512], F32, name="prm_ps", tag="xt")
-            nc.tensor.transpose(prm_ps[:, 0:P], prm_f[:], ident[:])
-            prm = const.tile([P, 32], F32, name="prm")
-            nc.vector.tensor_copy(out=prm[:], in_=prm_ps[:, 0:32])
-            bb = const.tile([P, 8], F32, name="bb")
-            nc.vector.tensor_tensor(out=bb[:], in0=prm[:, 16:24], in1=prm[:, 0:8], op=ALU.mult)
-            dd = const.tile([P, 8], F32, name="dd")
-            nc.vector.tensor_scalar(out=dd[:], in0=prm[:, 8:16], scalar1=-1.0, scalar2=1.0, op0=ALU.mult, op1=ALU.add)
+        prm = const.tile([P, 32], F32, name="prm")
+        bb = const.tile([P, 8], F32, name="bb")
+        dd = const.tile([P, 8], F32, name="dd")
+        wgrp = const.tile([P, PARTS * 4 * D], BF16, name="wgrp", align_bytes=64)
+        wc = const.tile([P, PARTS * D], U32, name="wc", align_bytes=64)
+        ws = const.tile([P, PARTS * D], U8, name="ws", align_bytes=64)
 
-            wgrp = const.tile([P, PARTS * 4 * D], BF16, name="wgrp", align_bytes=64)
-            wc = const.tile([P, PARTS * D], U32, name="wc", align_bytes=64)
-            ws = const.tile([P, PARTS * D], U8, name="ws", align_bytes=64)
-            for g in range(PARTS):
-                dst = wgrp[:, g * 4 * D : (g + 1) * 4 * D].rearrange("p (c t) -> p c t", t=4)
-                src = wraw[:, g * 4 * D : (g + 1) * 4 * D].rearrange("p (t c) -> p c t", t=4)
-                if g == 0:
-                    nc.vector.tensor_copy(out=dst, in_=src)
-                else:
-                    nc.scalar.copy(out=dst, in_=src)
-            for g in range(PARTS):
-                nc.vector.quantize_mx(
-                    out=wc[:, g * D : (g + 1) * D].bitcast(FP8X4),
-                    scales=ws[:, g * D : (g + 1) * D],
-                    in_=wgrp[:, g * 4 * D : (g + 1) * 4 * D],
-                )
-
-            cst["prm"] = prm
-            cst["bb"] = bb
-            cst["dd"] = dd
-            cst["wc"] = wc
-            cst["ws"] = ws
-
-        cst = {}
         xn = {}
         xg = {}
         xc = {}
@@ -127,92 +93,120 @@ def tile_better_transformer_t_kernel(tc, x, weights, bias, gain, norm_bias, gamm
         ob = {}
         ots = {}
 
+        def params():
+            prm_ps = psum.tile([P, P], BF16, name="prm_ps", tag="xt")
+            nc.tensor.transpose(prm_ps[:], prm_bf[:], ident_bf[:])
+            nc.vector.tensor_copy(out=prm[:], in_=prm_ps[:, 0:32])
+
+        def params2():
+            nc.vector.tensor_tensor(out=bb[:], in0=prm[:, 16:24], in1=prm[:, 0:8], op=ALU.mult)
+            nc.vector.tensor_scalar(out=dd[:], in0=prm[:, 8:16], scalar1=-1.0, scalar2=1.0, op0=ALU.mult, op1=ALU.add)
+
+        def w_group(g, hf):
+            lo = hf * HC
+            nc.vector.tensor_copy(
+                out=wgrp[:].rearrange("p (g c t) -> p g c t", g=PARTS, t=4)[:, g, lo : lo + HC, :],
+                in_=wraw[:].rearrange("p (g t c) -> p g c t", g=PARTS, t=4)[:, g, lo : lo + HC, :],
+            )
+
+        def w_quant(g, hf):
+            c0 = g * D + hf * HC
+            nc.vector.quantize_mx(
+                out=wc[:, c0 : c0 + HC].bitcast(FP8X4),
+                scales=ws[:, c0 : c0 + HC],
+                in_=wgrp[:, 4 * c0 : 4 * (c0 + HC)],
+            )
+
         def norm_x(i, u, g=None):
             if i not in xn:
                 xn[i] = xnp.tile([P, JT * IN], BF16, name="xn")
-            dst = xn[i][:].rearrange("p (u j g w e) -> p u j g w e", u=2, j=JT, g=PARTS, e=2)[:, u]
-            src = x_sb[i][:].rearrange("p (j g w u e) -> p u j g w e", u=2, j=JT, g=PARTS, e=2)[:, u]
             if g is None:
                 dst = xn[i][:].rearrange("p (u a e) -> p u a e", u=2, e=2)[:, u]
                 src = x_sb[i][:].rearrange("p (a u e) -> p u a e", u=2, e=2)[:, u]
             else:
-                dst = dst[:, :, g]
-                src = src[:, :, g]
+                dst = xn[i][:].rearrange("p (u j g w e) -> p u g j w e", u=2, j=JT, g=PARTS, e=2)[:, u, g]
+                src = x0[g][:].rearrange("p (j w u e) -> p u j w e", u=2, j=JT, e=2)[:, u]
             nc.vector.tensor_scalar(
-                out=dst, in0=src, scalar1=gain_f[:, 0:1], scalar2=nb_f[:, 0:1], op0=ALU.mult, op1=ALU.add
+                out=dst, in0=src, scalar1=gain_bf[:, 0:1], scalar2=nb_bf[:, 0:1], op0=ALU.mult, op1=ALU.add
             )
 
-        def stage_a(h, jp):
+        def x_trans(h, jp):
             i, g = divmod(h, PARTS)
             xw = xn[i][:].bitcast(F32)
             if jp == 0:
                 xg[h] = work.tile([P, 4 * ROWS], BF16, name="xg", align_bytes=64)
-            if True:
-                xt = psum.tile([P, 512], F32, name="xt", tag="xt")
-                for u in range(2):
-                    for jj in range(2):
-                        j = 2 * jp + jj
-                        col = u * (JT * IN // 4) + (j * PARTS + g) * P
-                        nc.tensor.transpose(
-                            xt[:, u * 256 + jj * P : u * 256 + (jj + 1) * P], xw[:, col : col + P], ident[:]
-                        )
-                nc.scalar.copy(
-                    out=xg[h][:, jp * 1024 : (jp + 1) * 1024].bitcast(F32).rearrange("p (n u) -> p n u", u=2),
-                    in_=xt[:].rearrange("p (u n) -> p n u", u=2),
-                )
+            xt = psum.tile([P, 512], F32, name="xt", tag="xt")
+            for u in range(2):
+                for jj in range(2):
+                    j = 2 * jp + jj
+                    col = u * (JT * IN // 4) + (j * PARTS + g) * P
+                    nc.tensor.transpose(
+                        xt[:, u * 256 + jj * P : u * 256 + (jj + 1) * P], xw[:, col : col + P], ident[:]
+                    )
+            nc.scalar.copy(
+                out=xg[h][:, jp * 1024 : (jp + 1) * 1024].bitcast(F32).rearrange("p (n u) -> p n u", u=2),
+                in_=xt[:].rearrange("p (u n) -> p n u", u=2),
+            )
 
-        def stage_q(h):
+        def x_quant(h):
             xc[h] = work.tile([P, ROWS], U32, name="xc", align_bytes=64)
             xs[h] = work.tile([P, ROWS], U8, name="xs", align_bytes=64)
             nc.vector.quantize_mx(out=xc[h][:].bitcast(FP8X4), scales=xs[h][:], in_=xg[h][:])
 
-        def stage_mx(h, k):
-            g = h % PARTS
-            q = g * CC + k
+        def mx(h, k):
+            q = (h % PARTS) * CC + k
             a = psum.tile([P, ROWS], F32, name="acc", tag="acc", bufs=4)
             acc[(h, k)] = a
             nc.tensor.matmul_mx(
                 out=a[:],
-                lhsT=cst["wc"][:, q * P : (q + 1) * P].bitcast(FP8X4),
-                lhsT_scale=cst["ws"][:, q * P : (q + 1) * P],
+                lhsT=wc[:, q * P : (q + 1) * P].bitcast(FP8X4),
+                lhsT_scale=ws[:, q * P : (q + 1) * P],
                 rhs=xc[h][:].bitcast(FP8X4),
                 rhs_scale=xs[h][:],
                 start=True,
                 stop=True,
             )
+
+        def sig(h, k):
+            q = (h % PARTS) * CC + k
             s = work.tile([P, ROWS], F32, name="sg", bufs=4)
             nc.scalar.activation(
-                out=s[:], in_=a[:], func=ACT.Sigmoid, scale=cst["prm"][:, 16 + q : 17 + q], bias=cst["bb"][:, q : q + 1]
+                out=s[:], in_=acc[(h, k)][:], func=ACT.Sigmoid, scale=prm[:, 16 + q : 17 + q], bias=bb[:, q : q + 1]
             )
             m = work.tile([P, ROWS], F32, name="mm", bufs=8)
             mm[(h, k)] = m
             nc.gpsimd.tensor_scalar(
-                out=m[:], in0=s[:], scalar1=cst["dd"][:, q : q + 1], scalar2=cst["prm"][:, 8 + q : 9 + q], op0=ALU.mult, op1=ALU.add
+                out=m[:], in0=s[:], scalar1=dd[:, q : q + 1], scalar2=prm[:, 8 + q : 9 + q], op0=ALU.mult, op1=ALU.add
             )
 
-        def stage_prod(h, k):
+        def prod(h, k):
             q = (h % PARTS) * CC + k
             if k == 0:
                 op[h] = work.tile([P, CC * ROWS], F32, name="op")
             nc.vector.scalar_tensor_tensor(
                 out=op[h][:, k * ROWS : (k + 1) * ROWS],
                 in0=acc[(h, k)][:],
-                scalar=cst["prm"][:, q : q + 1],
+                scalar=prm[:, q : q + 1],
                 in1=mm[(h, k)][:],
                 op0=ALU.add,
                 op1=ALU.mult,
             )
 
+        def x_tile(h, j):
+            i, g = divmod(h, PARTS)
+            if i == 0:
+                return x0[g][:, j * D : (j + 1) * D]
+            return x_sb[i][:, j * IN + g * D : j * IN + (g + 1) * D]
+
         def on_pe(h, j):
             return j == 1 or (j == 3 and h % 2 == 1)
 
-        def stage_back(h, j):
-            i, g = divmod(h, PARTS)
+        def back(h, j):
             ot = psum.tile([P, D], F32, name="ot", tag="ot")
             ots[(h, j)] = ot
             if on_pe(h, j):
                 nc.tensor.matmul(
-                    ot[:], lhsT=ident_bf[:], rhs=x_sb[i][:, j * IN + g * D : j * IN + (g + 1) * D], start=True, stop=False
+                    ot[:], lhsT=ident_bf[:], rhs=x_tile(h, j), start=True, stop=False
                 )
             for k in range(CC):
                 nc.tensor.matmul(
@@ -223,10 +217,11 @@ def tile_better_transformer_t_kernel(tc, x, weights, bias, gain, norm_bias, gamm
                     start=not on_pe(h, j),
                     stop=not on_pe(h, j) or k == CC - 1,
                 )
+            if on_pe(h, j):
+                finish(h, j)
 
-        def stage_res(h, j):
-            i, g = divmod(h, PARTS)
-            if j == 0:
+        def finish(h, j):
+            if h not in ob:
                 ob[h] = work.tile([P, JT * D], F32, name="ob", bufs=4)
             if on_pe(h, j):
                 nc.scalar.copy(out=ob[h][:, j * D : (j + 1) * D], in_=ots[(h, j)][:])
@@ -234,49 +229,98 @@ def tile_better_transformer_t_kernel(tc, x, weights, bias, gain, norm_bias, gamm
                 nc.vector.tensor_tensor(
                     out=ob[h][:, j * D : (j + 1) * D],
                     in0=ots[(h, j)][:],
-                    in1=x_sb[i][:, j * IN + g * D : j * IN + (g + 1) * D],
+                    in1=x_tile(h, j),
                     op=ALU.add,
                 )
+
+        def store(h, j0, j1):
+            i, g = divmod(h, PARTS)
             dst = out[i * ROWS : (i + 1) * ROWS, g * D : (g + 1) * D].rearrange("(p j) c -> p j c", j=JT)
             src = ob[h][:].rearrange("p (j c) -> p j c", j=JT)
-            if h == NU - 1:
-                nc.sync.dma_start(out=dst[:, j : j + 1, :], in_=src[:, j : j + 1, :])
-            elif j == JT - 1:
-                nc.sync.dma_start(out=dst, in_=src)
+            nc.sync.dma_start(out=dst[:, j0:j1, :], in_=src[:, j0:j1, :])
 
         def ok(h):
             return 0 <= h < NU
 
-        def main_loop():
-            for h in range(-3, NU + 1):
-                if h == -3:
-                    for g in range(PARTS):
-                        for u in range(2):
-                            norm_x(0, u, g)
-                if ok(h + 2):
-                    stage_q(h + 2)
-                for k in range(CC):
-                    if ok(h):
-                        stage_prod(h, k)
-                    if ok(h + 1):
-                        stage_mx(h + 1, k)
-                    if ok(h - 1):
-                        stage_res(h - 1, k)
-                    if k == 2 and 2 <= h + 5 < NU:
-                        norm_x((h + 5) // 2, (h + 5) % 2)
-                    if k < 2:
-                        if ok(h - 1):
-                            stage_back(h - 1, k + 2)
-                        if ok(h + 3):
-                            stage_a(h + 3, k)
-                if ok(h):
-                    stage_back(h, 0)
-                    stage_back(h, 1)
-                if h == -3:
-                    prep()
+        def trans_at(n):
+            if n < 0:
+                return []
+            if n == 0:
+                return [4, 5]
+            return [n + 5]
 
-        if MANUAL:
-            with tc.manual_schedule():
-                main_loop()
-        else:
-            main_loop()
+        def norm_at(n):
+            r = []
+            for i in range(1, NBLK):
+                for u in range(2):
+                    if n == (0 if i == 1 else max(2, 4 * i - 8 + 2 * u)):
+                        r.append((i, u))
+            return r
+
+        def slot(n):
+            h, b = divmod(n, 2)
+            if ok(h):
+                prod(h, 2 * b)
+                prod(h, 2 * b + 1)
+            if n == 0:
+                w_group(1, 1)
+            if ok(h + 1):
+                mx(h + 1, 2 * b)
+                mx(h + 1, 2 * b + 1)
+                sig(h + 1, 2 * b)
+                sig(h + 1, 2 * b + 1)
+            if ok(h - 1):
+                if b == 0:
+                    finish(h - 1, 0)
+                    if h == NU:
+                        store(h - 1, 0, 2)
+                else:
+                    finish(h - 1, 2)
+                    if not on_pe(h - 1, 3):
+                        finish(h - 1, 3)
+                    store(h - 1, 2 if h == NU else 0, 4)
+            for i, u in norm_at(n):
+                norm_x(i, u)
+            if n == 0:
+                w_quant(1, 1)
+            for m in trans_at(n):
+                if ok(m // 2):
+                    x_trans(m // 2, m % 2)
+            if b == 1 and ok(h):
+                back(h, 0)
+                back(h, 1)
+            if b == 0 and ok(h - 1):
+                back(h - 1, 2)
+                back(h - 1, 3)
+            if b == 1 and ok(h + 2) and h >= 0:
+                x_quant(h + 2)
+
+        def head():
+            for u in range(2):
+                norm_x(0, u, 0)
+            x_trans(0, 0)
+            x_trans(0, 1)
+            w_group(0, 0)
+            for u in range(2):
+                norm_x(0, u, 1)
+            w_quant(0, 0)
+            params()
+            x_trans(1, 0)
+            x_quant(0)
+            params2()
+            w_group(0, 1)
+            slot(-2)
+            w_group(1, 0)
+            w_quant(0, 1)
+            x_trans(1, 1)
+            slot(-1)
+            w_quant(1, 0)
+            x_quant(1)
+
+        def main():
+            head()
+            for n in range(2 * NU + 2):
+                slot(n)
+
+        with tc.manual_schedule():
+            main()

@@ -94,7 +94,7 @@ def tile_better_transformer_t_kernel(tc, x, weights, bias, gain, norm_bias, gamm
         ots = {}
 
         def params():
-            prm_ps = psum.tile([P, P], BF16, name="prm_ps", tag="xt")
+            prm_ps = psum.tile([P, P], BF16, name="prm_ps", tag="ot")
             nc.tensor.transpose(prm_ps[:], prm_bf[:], ident_bf[:])
             nc.vector.tensor_copy(out=prm[:], in_=prm_ps[:, 0:32])
 
@@ -102,9 +102,9 @@ def tile_better_transformer_t_kernel(tc, x, weights, bias, gain, norm_bias, gamm
             nc.vector.tensor_tensor(out=bb[:], in0=prm[:, 16:24], in1=prm[:, 0:8], op=ALU.mult)
             nc.vector.tensor_scalar(out=dd[:], in0=prm[:, 8:16], scalar1=-1.0, scalar2=1.0, op0=ALU.mult, op1=ALU.add)
 
-        def w_group(g, hf):
+        def w_group(g, hf, copy):
             lo = hf * HC
-            nc.vector.tensor_copy(
+            copy(
                 out=wgrp[:].rearrange("p (g c t) -> p g c t", g=PARTS, t=4)[:, g, lo : lo + HC, :],
                 in_=wraw[:].rearrange("p (g t c) -> p g c t", g=PARTS, t=4)[:, g, lo : lo + HC, :],
             )
@@ -135,7 +135,10 @@ def tile_better_transformer_t_kernel(tc, x, weights, bias, gain, norm_bias, gamm
             xw = xn[i][:].bitcast(F32)
             if jp == 0:
                 xg[h] = work.tile([P, 4 * ROWS], BF16, name="xg", align_bytes=64)
-            xt = psum.tile([P, 512], F32, name="xt", tag="xt")
+            if h < 3 and jp == 1:
+                xt = psum.tile([P, 512], F32, name="xt", tag="ot")
+            else:
+                xt = psum.tile([P, 512], F32, name="xt", tag="xt", bufs=1)
             for u in range(2):
                 for jj in range(2):
                     j = 2 * jp + jj
@@ -155,7 +158,7 @@ def tile_better_transformer_t_kernel(tc, x, weights, bias, gain, norm_bias, gamm
 
         def mx(h, k):
             q = (h % PARTS) * CC + k
-            a = psum.tile([P, ROWS], F32, name="acc", tag="acc", bufs=4)
+            a = psum.tile([P, ROWS], F32, name="acc", tag="acc", bufs=5)
             acc[(h, k)] = a
             nc.tensor.matmul_mx(
                 out=a[:],
@@ -201,14 +204,16 @@ def tile_better_transformer_t_kernel(tc, x, weights, bias, gain, norm_bias, gamm
         def on_pe(h, j):
             return j == 1 or (j == 3 and h % 2 == 1)
 
-        def back(h, j):
-            ot = psum.tile([P, D], F32, name="ot", tag="ot")
-            ots[(h, j)] = ot
-            if on_pe(h, j):
+        def back(h, j, ks=range(CC), tag="ot"):
+            if ks[0] == 0:
+                ot = psum.tile([P, D], F32, name="ot", tag=tag, bufs=5 if tag == "acc" else 2)
+                ots[(h, j)] = ot
+            ot = ots[(h, j)]
+            if on_pe(h, j) and ks[0] == 0:
                 nc.tensor.matmul(
                     ot[:], lhsT=ident_bf[:], rhs=x_tile(h, j), start=True, stop=False
                 )
-            for k in range(CC):
+            for k in ks:
                 nc.tensor.matmul(
                     ot[:, k * P : (k + 1) * P],
                     lhsT=op[h][:, k * ROWS + j * P : k * ROWS + (j + 1) * P],
@@ -217,7 +222,7 @@ def tile_better_transformer_t_kernel(tc, x, weights, bias, gain, norm_bias, gamm
                     start=not on_pe(h, j),
                     stop=not on_pe(h, j) or k == CC - 1,
                 )
-            if on_pe(h, j):
+            if on_pe(h, j) and ks[-1] == CC - 1:
                 finish(h, j)
 
         def finish(h, j):
@@ -259,11 +264,26 @@ def tile_better_transformer_t_kernel(tc, x, weights, bias, gain, norm_bias, gamm
 
         def slot(n):
             h, b = divmod(n, 2)
+            last = h == NU - 1 and b == 1
             if ok(h):
                 prod(h, 2 * b)
+                if n == 0:
+                    x_quant(1)
+                if last:
+                    finish(h - 1, 2)
+                    finish(h - 1, 3)
                 prod(h, 2 * b + 1)
+            if last:
+                store(h - 1, 0, JT)
+                for j in range(JT):
+                    back(h, j, range(CC - 1), "acc" if j < 2 else "ot")
+                for j in range(JT):
+                    back(h, j, [CC - 1])
+                    if not on_pe(h, j):
+                        finish(h, j)
+                    store(h, j, j + 1)
             if n == 0:
-                w_group(1, 1)
+                w_group(1, 1, nc.vector.tensor_copy)
             if ok(h + 1):
                 mx(h + 1, 2 * b)
                 mx(h + 1, 2 * b + 1)
@@ -272,13 +292,11 @@ def tile_better_transformer_t_kernel(tc, x, weights, bias, gain, norm_bias, gamm
             if ok(h - 1):
                 if b == 0:
                     finish(h - 1, 0)
-                    if h == NU:
-                        store(h - 1, 0, 2)
-                else:
+                elif not last:
                     finish(h - 1, 2)
                     if not on_pe(h - 1, 3):
                         finish(h - 1, 3)
-                    store(h - 1, 2 if h == NU else 0, 4)
+                    store(h - 1, 0, JT)
             for i, u in norm_at(n):
                 norm_x(i, u)
             if n == 0:
@@ -286,7 +304,7 @@ def tile_better_transformer_t_kernel(tc, x, weights, bias, gain, norm_bias, gamm
             for m in trans_at(n):
                 if ok(m // 2):
                     x_trans(m // 2, m % 2)
-            if b == 1 and ok(h):
+            if b == 1 and ok(h) and not last:
                 back(h, 0)
                 back(h, 1)
             if b == 0 and ok(h - 1):
@@ -300,26 +318,25 @@ def tile_better_transformer_t_kernel(tc, x, weights, bias, gain, norm_bias, gamm
                 norm_x(0, u, 0)
             x_trans(0, 0)
             x_trans(0, 1)
-            w_group(0, 0)
+            w_group(0, 0, nc.vector.tensor_copy)
+            params()
+            w_quant(0, 0)
+            w_group(0, 1, nc.scalar.copy)
+            params2()
+            x_quant(0)
+            slot(-2)
             for u in range(2):
                 norm_x(0, u, 1)
-            w_quant(0, 0)
-            params()
-            x_trans(1, 0)
-            x_quant(0)
-            params2()
-            w_group(0, 1)
-            slot(-2)
-            w_group(1, 0)
             w_quant(0, 1)
+            x_trans(1, 0)
             x_trans(1, 1)
+            w_group(1, 0, nc.vector.tensor_copy)
             slot(-1)
             w_quant(1, 0)
-            x_quant(1)
 
         def main():
             head()
-            for n in range(2 * NU + 2):
+            for n in range(2 * NU):
                 slot(n)
 
         with tc.manual_schedule():

@@ -34,10 +34,12 @@ def tile_better_transformer_t_kernel(tc, x, weights, bias, gain, norm_bias, gamm
         work = ctx.enter_context(tc.tile_pool(name="work", bufs=3))
         psum = ctx.enter_context(tc.psum_pool(name="psum", bufs=2))
 
-        gain_bf = const.tile([P, 1], BF16, name="gain_bf")
-        nb_bf = const.tile([P, 1], BF16, name="nb_bf")
-        nc.sync.dma_start(out=gain_bf[:], in_=gain.partition_broadcast(P))
-        nc.scalar.dma_start(out=nb_bf[:], in_=norm_bias.partition_broadcast(P))
+        gn_bf = const.tile([P, 32], BF16, name="gn_bf")
+        nc.vector.memset(gn_bf[:], 0.0)
+        nc.sync.dma_start(out=gn_bf[0:1, 0:1], in_=gain.rearrange("(o k) -> o k", o=1))
+        nc.sync.dma_start(out=gn_bf[0:1, 16:17], in_=norm_bias.rearrange("(o k) -> o k", o=1))
+        ones = const.tile([P, P], BF16, name="ones")
+        nc.gpsimd.memset(ones[:], 1.0)
         prm_bf = const.tile([P, P], BF16, name="prm_bf")
         nc.vector.memset(prm_bf[:], 0.0)
         nc.scalar.dma_start(out=prm_bf[0:8, :], in_=bias.rearrange("(r c) -> r c", c=P))
@@ -76,6 +78,10 @@ def tile_better_transformer_t_kernel(tc, x, weights, bias, gain, norm_bias, gamm
         ident_bf = const.tile([P, P], BF16, name="ident_bf")
         nc.vector.tensor_copy(out=ident_bf[:], in_=ident[:])
 
+        gn = const.tile([P, 32], F32, name="gn")
+        gn_ps = psum.tile([P, 32], F32, name="gn_ps", tag="ot")
+        nc.tensor.matmul(gn_ps[:], lhsT=ones[:], rhs=gn_bf[:], start=True, stop=True)
+        nc.vector.tensor_copy(out=gn[:], in_=gn_ps[:])
         prm = const.tile([P, 32], F32, name="prm")
         bb = const.tile([P, 8], F32, name="bb")
         dd = const.tile([P, 8], F32, name="dd")
@@ -125,14 +131,21 @@ def tile_better_transformer_t_kernel(tc, x, weights, bias, gain, norm_bias, gamm
                 src = x_sb[i][:].rearrange("p (a u e) -> p u a e", u=2, e=2)[:, u]
             else:
                 dst = xn[i][:].rearrange("p (u j g w e) -> p u g j w e", u=2, j=JT, g=PARTS, e=2)[:, u, g]
-                src = x0[g][:].rearrange("p (j w u e) -> p u j w e", u=2, j=JT, e=2)[:, u]
+                if i == 0:
+                    src = x0[g][:].rearrange("p (j w u e) -> p u j w e", u=2, j=JT, e=2)[:, u]
+                else:
+                    src = x_sb[i][:].rearrange("p (j g w u e) -> p u g j w e", u=2, j=JT, g=PARTS, e=2)[:, u, g]
             nc.vector.tensor_scalar(
-                out=dst, in0=src, scalar1=gain_bf[:, 0:1], scalar2=nb_bf[:, 0:1], op0=ALU.mult, op1=ALU.add
+                out=dst, in0=src, scalar1=gn[:, 0:1], scalar2=gn[:, 16:17], op0=ALU.mult, op1=ALU.add
             )
+
+        def by_scalar(h):
+            i, g = divmod(h, PARTS)
+            return g == 1 and i % 2 == 1
 
         def x_trans(h, jp):
             i, g = divmod(h, PARTS)
-            xw = xn[i][:].bitcast(F32)
+            xw = x_sb[i][:].bitcast(F32) if by_scalar(h) else xn[i][:].bitcast(F32)
             if jp == 0:
                 xg[h] = work.tile([P, 4 * ROWS], BF16, name="xg", align_bytes=64)
             if h < 3 and jp == 1:
@@ -142,14 +155,27 @@ def tile_better_transformer_t_kernel(tc, x, weights, bias, gain, norm_bias, gamm
             for u in range(2):
                 for jj in range(2):
                     j = 2 * jp + jj
-                    col = u * (JT * IN // 4) + (j * PARTS + g) * P
-                    nc.tensor.transpose(
-                        xt[:, u * 256 + jj * P : u * 256 + (jj + 1) * P], xw[:, col : col + P], ident[:]
-                    )
-            nc.scalar.copy(
-                out=xg[h][:, jp * 1024 : (jp + 1) * 1024].bitcast(F32).rearrange("p (n u) -> p n u", u=2),
-                in_=xt[:].rearrange("p (u n) -> p n u", u=2),
-            )
+                    if by_scalar(h):
+                        col = j * (IN // 2) + g * (D // 2)
+                        words = xw[:, col + u : col + D // 2 : 2]
+                    else:
+                        col = u * (JT * IN // 4) + (j * PARTS + g) * P
+                        words = xw[:, col : col + P]
+                    nc.tensor.transpose(xt[:, u * 256 + jj * P : u * 256 + (jj + 1) * P], words, ident[:])
+            xg_h = xg[h][:, jp * 1024 : (jp + 1) * 1024]
+            if by_scalar(h):
+                nc.scalar.activation(
+                    out=xg_h.rearrange("p (n u e) -> p n u e", u=2, e=2),
+                    in_=xt[:].bitcast(BF16).rearrange("p (u n e) -> p n u e", u=2, e=2),
+                    func=ACT.Identity,
+                    scale=gn[:, 0:1],
+                    bias=gn[:, 16:17],
+                )
+            else:
+                nc.scalar.copy(
+                    out=xg_h.bitcast(F32).rearrange("p (n u) -> p n u", u=2),
+                    in_=xt[:].rearrange("p (u n) -> p n u", u=2),
+                )
 
         def x_quant(h):
             xc[h] = work.tile([P, ROWS], U32, name="xc", align_bytes=64)
@@ -269,8 +295,9 @@ def tile_better_transformer_t_kernel(tc, x, weights, bias, gain, norm_bias, gamm
                 prod(h, 2 * b)
                 if n == 0:
                     x_quant(1)
+                if ok(h - 1):
+                    finish(h - 1, 2 * b)
                 if last:
-                    finish(h - 1, 2)
                     finish(h - 1, 3)
                 prod(h, 2 * b + 1)
             if last:
@@ -289,16 +316,12 @@ def tile_better_transformer_t_kernel(tc, x, weights, bias, gain, norm_bias, gamm
                 mx(h + 1, 2 * b + 1)
                 sig(h + 1, 2 * b)
                 sig(h + 1, 2 * b + 1)
-            if ok(h - 1):
-                if b == 0:
-                    finish(h - 1, 0)
-                elif not last:
-                    finish(h - 1, 2)
-                    if not on_pe(h - 1, 3):
-                        finish(h - 1, 3)
-                    store(h - 1, 0, JT)
+            if b == 1 and ok(h - 1) and not last:
+                if not on_pe(h - 1, 3):
+                    finish(h - 1, 3)
+                store(h - 1, 0, JT)
             for i, u in norm_at(n):
-                norm_x(i, u)
+                norm_x(i, u, 0 if by_scalar(2 * i + 1) else None)
             if n == 0:
                 w_quant(1, 1)
             for m in trans_at(n):

@@ -123,7 +123,7 @@ def tile_better_transformer_t_kernel(tc, x, weights, bias, gain, norm_bias, gamm
                 in_=wgrp[:, 4 * c0 : 4 * (c0 + HC)],
             )
 
-        def norm_x(i, u, g=None):
+        def norm_x(i, u, g=None, j0=0, j1=JT):
             if i not in xn:
                 xn[i] = xnp.tile([P, JT * IN], BF16, name="xn")
             if g is None:
@@ -131,8 +131,9 @@ def tile_better_transformer_t_kernel(tc, x, weights, bias, gain, norm_bias, gamm
                 src = x_sb[i][:].rearrange("p (a u e) -> p u a e", u=2, e=2)[:, u]
             else:
                 dst = xn[i][:].rearrange("p (u j g w e) -> p u g j w e", u=2, j=JT, g=PARTS, e=2)[:, u, g]
+                dst = dst[:, j0:j1]
                 if i == 0:
-                    src = x0[g][:].rearrange("p (j w u e) -> p u j w e", u=2, j=JT, e=2)[:, u]
+                    src = x0[g][:].rearrange("p (j w u e) -> p u j w e", u=2, j=JT, e=2)[:, u, j0:j1]
                 else:
                     src = x_sb[i][:].rearrange("p (j g w u e) -> p u g j w e", u=2, j=JT, g=PARTS, e=2)[:, u, g]
             nc.vector.tensor_scalar(
@@ -177,10 +178,13 @@ def tile_better_transformer_t_kernel(tc, x, weights, bias, gain, norm_bias, gamm
                     in_=xt[:].rearrange("p (u n) -> p n u", u=2),
                 )
 
-        def x_quant(h):
-            xc[h] = work.tile([P, ROWS], U32, name="xc", align_bytes=64)
-            xs[h] = work.tile([P, ROWS], U8, name="xs", align_bytes=64)
-            nc.vector.quantize_mx(out=xc[h][:].bitcast(FP8X4), scales=xs[h][:], in_=xg[h][:])
+        def x_quant(h, lo=0, hi=ROWS):
+            if lo == 0:
+                xc[h] = work.tile([P, ROWS], U32, name="xc", align_bytes=64)
+                xs[h] = work.tile([P, ROWS], U8, name="xs", align_bytes=64)
+            nc.vector.quantize_mx(
+                out=xc[h][:, lo:hi].bitcast(FP8X4), scales=xs[h][:, lo:hi], in_=xg[h][:, 4 * lo : 4 * hi]
+            )
 
         def mx(h, k):
             q = (h % PARTS) * CC + k
@@ -198,7 +202,7 @@ def tile_better_transformer_t_kernel(tc, x, weights, bias, gain, norm_bias, gamm
 
         def sig(h, k):
             q = (h % PARTS) * CC + k
-            s = work.tile([P, ROWS], F32, name="sg", bufs=4)
+            s = work.tile([P, ROWS], F32, name="sg", bufs=5)
             nc.scalar.activation(
                 out=s[:], in_=acc[(h, k)][:], func=ACT.Sigmoid, scale=prm[:, 16 + q : 17 + q], bias=bb[:, q : q + 1]
             )
@@ -208,15 +212,15 @@ def tile_better_transformer_t_kernel(tc, x, weights, bias, gain, norm_bias, gamm
                 out=m[:], in0=s[:], scalar1=dd[:, q : q + 1], scalar2=prm[:, 8 + q : 9 + q], op0=ALU.mult, op1=ALU.add
             )
 
-        def prod(h, k):
+        def prod(h, k, lo=0, hi=ROWS):
             q = (h % PARTS) * CC + k
             if k == 0:
                 op[h] = work.tile([P, CC * ROWS], F32, name="op")
             nc.vector.scalar_tensor_tensor(
-                out=op[h][:, k * ROWS : (k + 1) * ROWS],
-                in0=acc[(h, k)][:],
+                out=op[h][:, k * ROWS + lo : k * ROWS + hi],
+                in0=acc[(h, k)][:, lo:hi],
                 scalar=prm[:, q : q + 1],
-                in1=mm[(h, k)][:],
+                in1=mm[(h, k)][:, lo:hi],
                 op0=ALU.add,
                 op1=ALU.mult,
             )
@@ -228,7 +232,7 @@ def tile_better_transformer_t_kernel(tc, x, weights, bias, gain, norm_bias, gamm
             return x_sb[i][:, j * IN + g * D : j * IN + (g + 1) * D]
 
         def on_pe(h, j):
-            return j == 1 or (j == 3 and h % 2 == 1)
+            return j == 1 or (j == 3 and (h % 2 == 1 or h == NU - 2))
 
         def back(h, j, ks=range(CC), tag="ot"):
             if ks[0] == 0:
@@ -295,22 +299,29 @@ def tile_better_transformer_t_kernel(tc, x, weights, bias, gain, norm_bias, gamm
                 prod(h, 2 * b)
                 if n == 0:
                     x_quant(1)
-                if ok(h - 1):
+                if n == 2:
+                    x_quant(2)
+                if ok(h - 1) and not last:
                     finish(h - 1, 2 * b)
-                if last:
-                    finish(h - 1, 3)
-                prod(h, 2 * b + 1)
+                    if b == 0:
+                        store(h - 1, 0, 2)
+                if not last:
+                    prod(h, 2 * b + 1)
             if last:
-                store(h - 1, 0, JT)
-                for j in range(JT):
-                    back(h, j, range(CC - 1), "acc" if j < 2 else "ot")
-                for j in range(JT):
+                prod(h, CC - 1, 0, ROWS // 2)
+                prod(h, CC - 1, ROWS // 2, ROWS)
+                store(h - 1, 3, JT)
+                finish(h - 1, 2)
+                store(h - 1, 2, 3)
+                for j in range(JT - 1):
+                    back(h, j, range(CC - 1), "acc")
+                for j in range(JT - 1):
                     back(h, j, [CC - 1])
+                back(h, JT - 1)
+                for j in range(JT):
                     if not on_pe(h, j):
                         finish(h, j)
                     store(h, j, j + 1)
-            if n == 0:
-                w_group(1, 1, nc.vector.tensor_copy)
             if ok(h + 1):
                 mx(h + 1, 2 * b)
                 mx(h + 1, 2 * b + 1)
@@ -319,11 +330,9 @@ def tile_better_transformer_t_kernel(tc, x, weights, bias, gain, norm_bias, gamm
             if b == 1 and ok(h - 1) and not last:
                 if not on_pe(h - 1, 3):
                     finish(h - 1, 3)
-                store(h - 1, 0, JT)
+                store(h - 1, 2, JT)
             for i, u in norm_at(n):
                 norm_x(i, u, 0 if by_scalar(2 * i + 1) else None)
-            if n == 0:
-                w_quant(1, 1)
             for m in trans_at(n):
                 if ok(m // 2):
                     x_trans(m // 2, m % 2)
@@ -333,20 +342,21 @@ def tile_better_transformer_t_kernel(tc, x, weights, bias, gain, norm_bias, gamm
             if b == 0 and ok(h - 1):
                 back(h - 1, 2)
                 back(h - 1, 3)
-            if b == 1 and ok(h + 2) and h >= 0:
+            if b == 1 and ok(h + 2) and h > 0:
                 x_quant(h + 2)
 
         def head():
-            for u in range(2):
-                norm_x(0, u, 0)
-            x_trans(0, 0)
-            x_trans(0, 1)
+            for jp in range(2):
+                for u in range(2):
+                    norm_x(0, u, 0, 2 * jp, 2 * jp + 2)
+                x_trans(0, jp)
             w_group(0, 0, nc.vector.tensor_copy)
-            params()
+            w_group(0, 1, nc.vector.tensor_copy)
             w_quant(0, 0)
-            w_group(0, 1, nc.scalar.copy)
+            params()
             params2()
-            x_quant(0)
+            x_quant(0, 0, ROWS // 2)
+            x_quant(0, ROWS // 2, ROWS)
             slot(-2)
             for u in range(2):
                 norm_x(0, u, 1)
@@ -354,8 +364,10 @@ def tile_better_transformer_t_kernel(tc, x, weights, bias, gain, norm_bias, gamm
             x_trans(1, 0)
             x_trans(1, 1)
             w_group(1, 0, nc.vector.tensor_copy)
+            w_group(1, 1, nc.vector.tensor_copy)
             slot(-1)
             w_quant(1, 0)
+            w_quant(1, 1)
 
         def main():
             head()

@@ -263,8 +263,8 @@ def tile_better_transformer_t_kernel(tc, x, weights, bias, gain, norm_bias, gamm
             else:
                 nc.vector.tensor_tensor(
                     out=ob[h][:, j * D : (j + 1) * D],
-                    in0=ots[(h, j)][:],
-                    in1=x_tile(h, j),
+                    in0=x_tile(h, j),
+                    in1=ots[(h, j)][:],
                     op=ALU.add,
                 )
 
@@ -298,12 +298,14 @@ def tile_better_transformer_t_kernel(tc, x, weights, bias, gain, norm_bias, gamm
             if ok(h):
                 prod(h, 2 * b)
                 if n == 0:
+                    w_quant(1, 0)
                     x_quant(1)
+                    w_quant(1, 1)
                 if n == 2:
                     x_quant(2)
                 if ok(h - 1) and not last:
                     finish(h - 1, 2 * b)
-                    if b == 0:
+                    if b == 0 and h == NU - 1:
                         store(h - 1, 0, 2)
                 if not last:
                     prod(h, 2 * b + 1)
@@ -330,7 +332,7 @@ def tile_better_transformer_t_kernel(tc, x, weights, bias, gain, norm_bias, gamm
             if b == 1 and ok(h - 1) and not last:
                 if not on_pe(h - 1, 3):
                     finish(h - 1, 3)
-                store(h - 1, 2, JT)
+                store(h - 1, 0, JT)
             for i, u in norm_at(n):
                 norm_x(i, u, 0 if by_scalar(2 * i + 1) else None)
             for m in trans_at(n):
@@ -351,9 +353,9 @@ def tile_better_transformer_t_kernel(tc, x, weights, bias, gain, norm_bias, gamm
                     norm_x(0, u, 0, 2 * jp, 2 * jp + 2)
                 x_trans(0, jp)
             w_group(0, 0, nc.vector.tensor_copy)
-            w_group(0, 1, nc.vector.tensor_copy)
-            w_quant(0, 0)
             params()
+            w_quant(0, 0)
+            w_group(0, 1, nc.scalar.copy)
             params2()
             x_quant(0, 0, ROWS // 2)
             x_quant(0, ROWS // 2, ROWS)
@@ -366,8 +368,6 @@ def tile_better_transformer_t_kernel(tc, x, weights, bias, gain, norm_bias, gamm
             w_group(1, 0, nc.vector.tensor_copy)
             w_group(1, 1, nc.vector.tensor_copy)
             slot(-1)
-            w_quant(1, 0)
-            w_quant(1, 1)
 
         def main():
             head()

@@ -30,7 +30,6 @@ def tile_better_transformer_t_kernel(tc, x, weights, bias, gain, norm_bias, gamm
     with ExitStack() as ctx:
         const = ctx.enter_context(tc.tile_pool(name="const", bufs=1))
         xin = ctx.enter_context(tc.tile_pool(name="xin", bufs=NBLK - 1))
-        xnp = ctx.enter_context(tc.tile_pool(name="xnp", bufs=3))
         work = ctx.enter_context(tc.tile_pool(name="work", bufs=3))
         psum = ctx.enter_context(tc.psum_pool(name="psum", bufs=2))
 
@@ -89,11 +88,13 @@ def tile_better_transformer_t_kernel(tc, x, weights, bias, gain, norm_bias, gamm
         wc = const.tile([P, PARTS * D], U32, name="wc", align_bytes=64)
         ws = const.tile([P, PARTS * D], U8, name="ws", align_bytes=64)
 
-        xn = {}
+        xn0 = const.tile([P, JT * IN], BF16, name="xn0")
+        late = []
         xg = {}
         xc = {}
         xs = {}
         acc = {}
+        sg = {}
         mm = {}
         op = {}
         ob = {}
@@ -123,32 +124,18 @@ def tile_better_transformer_t_kernel(tc, x, weights, bias, gain, norm_bias, gamm
                 in_=wgrp[:, 4 * c0 : 4 * (c0 + HC)],
             )
 
-        def norm_x(i, u, g=None, j0=0, j1=JT):
-            if i not in xn:
-                xn[i] = xnp.tile([P, JT * IN], BF16, name="xn")
-            if g is None:
-                dst = xn[i][:].rearrange("p (u a e) -> p u a e", u=2, e=2)[:, u]
-                src = x_sb[i][:].rearrange("p (a u e) -> p u a e", u=2, e=2)[:, u]
-            else:
-                dst = xn[i][:].rearrange("p (u j g w e) -> p u g j w e", u=2, j=JT, g=PARTS, e=2)[:, u, g]
-                dst = dst[:, j0:j1]
-                if i == 0:
-                    src = x0[g][:].rearrange("p (j w u e) -> p u j w e", u=2, j=JT, e=2)[:, u, j0:j1]
-                else:
-                    src = x_sb[i][:].rearrange("p (j g w u e) -> p u g j w e", u=2, j=JT, g=PARTS, e=2)[:, u, g]
+        def norm_x(u, g, j0=0, j1=JT):
+            dst = xn0[:].rearrange("p (u j g w e) -> p u g j w e", u=2, j=JT, g=PARTS, e=2)[:, u, g, j0:j1]
+            src = x0[g][:].rearrange("p (j w u e) -> p u j w e", u=2, j=JT, e=2)[:, u, j0:j1]
             nc.vector.tensor_scalar(
                 out=dst, in0=src, scalar1=gn[:, 0:1], scalar2=gn[:, 16:17], op0=ALU.mult, op1=ALU.add
             )
 
-        def by_scalar(h):
-            i, g = divmod(h, PARTS)
-            return g == 1 and i % 2 == 1
-
         def x_trans(h, jp):
             i, g = divmod(h, PARTS)
-            xw = x_sb[i][:].bitcast(F32) if by_scalar(h) else xn[i][:].bitcast(F32)
+            xw = (xn0 if i == 0 else x_sb[i])[:].bitcast(F32)
             if jp == 0:
-                xg[h] = work.tile([P, 4 * ROWS], BF16, name="xg", align_bytes=64)
+                xg[h] = work.tile([P, 4 * ROWS], BF16, name="xg", bufs=4, align_bytes=64)
             if h < 3 and jp == 1:
                 xt = psum.tile([P, 512], F32, name="xt", tag="ot")
             else:
@@ -156,26 +143,32 @@ def tile_better_transformer_t_kernel(tc, x, weights, bias, gain, norm_bias, gamm
             for u in range(2):
                 for jj in range(2):
                     j = 2 * jp + jj
-                    if by_scalar(h):
-                        col = j * (IN // 2) + g * (D // 2)
-                        words = xw[:, col + u : col + D // 2 : 2]
-                    else:
+                    if i == 0:
                         col = u * (JT * IN // 4) + (j * PARTS + g) * P
                         words = xw[:, col : col + P]
+                    else:
+                        col = j * (IN // 2) + g * (D // 2)
+                        words = xw[:, col + u : col + D // 2 : 2]
                     nc.tensor.transpose(xt[:, u * 256 + jj * P : u * 256 + (jj + 1) * P], words, ident[:])
             xg_h = xg[h][:, jp * 1024 : (jp + 1) * 1024]
-            if by_scalar(h):
-                nc.scalar.activation(
-                    out=xg_h.rearrange("p (n u e) -> p n u e", u=2, e=2),
-                    in_=xt[:].bitcast(BF16).rearrange("p (u n e) -> p n u e", u=2, e=2),
-                    func=ACT.Identity,
-                    scale=gn[:, 0:1],
-                    bias=gn[:, 16:17],
-                )
-            else:
+            if i == 0:
                 nc.scalar.copy(
                     out=xg_h.bitcast(F32).rearrange("p (n u) -> p n u", u=2),
                     in_=xt[:].rearrange("p (u n) -> p n u", u=2),
+                )
+                return
+            dst = xg_h.rearrange("p (n u e) -> p n u e", u=2, e=2)
+            src = xt[:].bitcast(BF16).rearrange("p (u n e) -> p n u e", u=2, e=2)
+            if jp == 0:
+                late.append((dst, src))
+            else:
+                nc.scalar.activation(out=dst, in_=src, func=ACT.Identity, scale=gn[:, 0:1], bias=gn[:, 16:17])
+
+        def x_late():
+            while late:
+                dst, src = late.pop(0)
+                nc.vector.tensor_scalar(
+                    out=dst, in0=src, scalar1=gn[:, 0:1], scalar2=gn[:, 16:17], op0=ALU.mult, op1=ALU.add
                 )
 
         def x_quant(h, lo=0, hi=ROWS):
@@ -206,10 +199,21 @@ def tile_better_transformer_t_kernel(tc, x, weights, bias, gain, norm_bias, gamm
             nc.scalar.activation(
                 out=s[:], in_=acc[(h, k)][:], func=ACT.Sigmoid, scale=prm[:, 16 + q : 17 + q], bias=bb[:, q : q + 1]
             )
+            sg[(h, k)] = s
+            if h > 0:
+                mult(h, k, nc.gpsimd)
+
+        def mult(h, k, eng):
+            q = (h % PARTS) * CC + k
             m = work.tile([P, ROWS], F32, name="mm", bufs=8)
             mm[(h, k)] = m
-            nc.gpsimd.tensor_scalar(
-                out=m[:], in0=s[:], scalar1=dd[:, q : q + 1], scalar2=prm[:, 8 + q : 9 + q], op0=ALU.mult, op1=ALU.add
+            eng.tensor_scalar(
+                out=m[:],
+                in0=sg[(h, k)][:],
+                scalar1=dd[:, q : q + 1],
+                scalar2=prm[:, 8 + q : 9 + q],
+                op0=ALU.mult,
+                op1=ALU.add,
             )
 
         def prod(h, k, lo=0, hi=ROWS):
@@ -234,6 +238,9 @@ def tile_better_transformer_t_kernel(tc, x, weights, bias, gain, norm_bias, gamm
         def on_pe(h, j):
             return j == 1 or (j == 3 and (h % 2 == 1 or h == NU - 2))
 
+        def on_gpsimd(h, j):
+            return j == 3 and h % 2 == 0 and 2 <= h <= 12
+
         def back(h, j, ks=range(CC), tag="ot"):
             if ks[0] == 0:
                 ot = psum.tile([P, D], F32, name="ot", tag=tag, bufs=5 if tag == "acc" else 2)
@@ -252,17 +259,20 @@ def tile_better_transformer_t_kernel(tc, x, weights, bias, gain, norm_bias, gamm
                     start=not on_pe(h, j),
                     stop=not on_pe(h, j) or k == CC - 1,
                 )
-            if on_pe(h, j) and ks[-1] == CC - 1:
+            if (on_pe(h, j) or on_gpsimd(h, j)) and ks[-1] == CC - 1:
                 finish(h, j)
 
         def finish(h, j):
             if h not in ob:
                 ob[h] = work.tile([P, JT * D], F32, name="ob", bufs=4)
-            if on_pe(h, j):
-                nc.scalar.copy(out=ob[h][:, j * D : (j + 1) * D], in_=ots[(h, j)][:])
+            dst = ob[h][:, j * D : (j + 1) * D]
+            if on_pe(h, j) or on_gpsimd(h, j):
+                nc.scalar.copy(out=dst, in_=ots[(h, j)][:])
+                if on_gpsimd(h, j):
+                    nc.gpsimd.tensor_tensor(out=dst, in0=dst, in1=x_tile(h, j), op=ALU.add)
             else:
                 nc.vector.tensor_tensor(
-                    out=ob[h][:, j * D : (j + 1) * D],
+                    out=dst,
                     in0=x_tile(h, j),
                     in1=ots[(h, j)][:],
                     op=ALU.add,
@@ -284,18 +294,13 @@ def tile_better_transformer_t_kernel(tc, x, weights, bias, gain, norm_bias, gamm
                 return [4, 5]
             return [n + 5]
 
-        def norm_at(n):
-            r = []
-            for i in range(1, NBLK):
-                for u in range(2):
-                    if n == (0 if i == 1 else max(2, 4 * i - 8 + 2 * u)):
-                        r.append((i, u))
-            return r
-
         def slot(n):
             h, b = divmod(n, 2)
             last = h == NU - 1 and b == 1
             if ok(h):
+                if h == 0:
+                    mult(h, 2 * b, nc.vector)
+                    mult(h, 2 * b + 1, nc.vector)
                 prod(h, 2 * b)
                 if n == 0:
                     w_quant(1, 0)
@@ -303,6 +308,7 @@ def tile_better_transformer_t_kernel(tc, x, weights, bias, gain, norm_bias, gamm
                     w_quant(1, 1)
                 if n == 2:
                     x_quant(2)
+                x_late()
                 if ok(h - 1) and not last:
                     finish(h - 1, 2 * b)
                     if b == 0 and h == NU - 1:
@@ -330,11 +336,9 @@ def tile_better_transformer_t_kernel(tc, x, weights, bias, gain, norm_bias, gamm
                 sig(h + 1, 2 * b)
                 sig(h + 1, 2 * b + 1)
             if b == 1 and ok(h - 1) and not last:
-                if not on_pe(h - 1, 3):
+                if not on_pe(h - 1, 3) and not on_gpsimd(h - 1, 3):
                     finish(h - 1, 3)
                 store(h - 1, 0, JT)
-            for i, u in norm_at(n):
-                norm_x(i, u, 0 if by_scalar(2 * i + 1) else None)
             for m in trans_at(n):
                 if ok(m // 2):
                     x_trans(m // 2, m % 2)
@@ -350,7 +354,7 @@ def tile_better_transformer_t_kernel(tc, x, weights, bias, gain, norm_bias, gamm
         def head():
             for jp in range(2):
                 for u in range(2):
-                    norm_x(0, u, 0, 2 * jp, 2 * jp + 2)
+                    norm_x(u, 0, 2 * jp, 2 * jp + 2)
                 x_trans(0, jp)
             w_group(0, 0, nc.vector.tensor_copy)
             params()
@@ -361,7 +365,7 @@ def tile_better_transformer_t_kernel(tc, x, weights, bias, gain, norm_bias, gamm
             x_quant(0, ROWS // 2, ROWS)
             slot(-2)
             for u in range(2):
-                norm_x(0, u, 1)
+                norm_x(u, 1)
             w_quant(0, 1)
             x_trans(1, 0)
             x_trans(1, 1)

@@ -22,6 +22,7 @@ NBLK = B // ROWS
 NU = NBLK * PARTS
 CC = D // P
 HC = D // 2
+FINE = NU - 4
 FLOPS = 2 * B * D * D * PARTS
 
 
@@ -219,7 +220,7 @@ def tile_better_transformer_t_kernel(tc, x, weights, bias, gain, norm_bias, gamm
         def prod(h, k, lo=0, hi=ROWS):
             q = (h % PARTS) * CC + k
             if k == 0:
-                op[h] = work.tile([P, CC * ROWS], F32, name="op")
+                op[h] = work.tile([P, CC * ROWS], F32, name="op", bufs=4)
             nc.vector.scalar_tensor_tensor(
                 out=op[h][:, k * ROWS + lo : k * ROWS + hi],
                 in0=acc[(h, k)][:, lo:hi],
@@ -264,7 +265,7 @@ def tile_better_transformer_t_kernel(tc, x, weights, bias, gain, norm_bias, gamm
 
         def finish(h, j):
             if h not in ob:
-                ob[h] = work.tile([P, JT * D], F32, name="ob", bufs=4)
+                ob[h] = work.tile([P, JT * D], F32, name="ob", bufs=7)
             dst = ob[h][:, j * D : (j + 1) * D]
             if on_pe(h, j) or on_gpsimd(h, j):
                 nc.scalar.copy(out=dst, in_=ots[(h, j)][:])
@@ -311,7 +312,7 @@ def tile_better_transformer_t_kernel(tc, x, weights, bias, gain, norm_bias, gamm
                 x_late()
                 if ok(h - 1) and not last:
                     finish(h - 1, 2 * b)
-                    if b == 0 and h == NU - 1:
+                    if b == 0 and h > FINE:
                         store(h - 1, 0, 2)
                 if not last:
                     prod(h, 2 * b + 1)
@@ -338,7 +339,7 @@ def tile_better_transformer_t_kernel(tc, x, weights, bias, gain, norm_bias, gamm
             if b == 1 and ok(h - 1) and not last:
                 if not on_pe(h - 1, 3) and not on_gpsimd(h - 1, 3):
                     finish(h - 1, 3)
-                store(h - 1, 0, JT)
+                store(h - 1, 2 if h > FINE else 0, JT)
             for m in trans_at(n):
                 if ok(m // 2):
                     x_trans(m // 2, m % 2)

@@ -36,8 +36,6 @@ def tile_better_transformer_t_kernel(tc, x, weights, bias, gain, norm_bias, gamm
 
         gn_bf = const.tile([P, 32], BF16, name="gn_bf")
         nc.vector.memset(gn_bf[:], 0.0)
-        nc.sync.dma_start(out=gn_bf[0:1, 0:1], in_=gain.rearrange("(o k) -> o k", o=1))
-        nc.sync.dma_start(out=gn_bf[0:1, 16:17], in_=norm_bias.rearrange("(o k) -> o k", o=1))
         ones = const.tile([P, P], BF16, name="ones")
         nc.gpsimd.memset(ones[:], 1.0)
         prm_bf = const.tile([P, P], BF16, name="prm_bf")
@@ -51,22 +49,36 @@ def tile_better_transformer_t_kernel(tc, x, weights, bias, gain, norm_bias, gamm
 
         x0 = []
         for g in range(PARTS):
-            x0_g = const.tile([P, JT * D], BF16, name="x0_%d" % g)
-            x0.append(x0_g)
+            x0.append([])
+            for jp in range(2):
+                x0_gj = const.tile([P, 2 * D], BF16, name="x0_%d%d" % (g, jp))
+                x0[g].append(x0_gj)
         x_sb = [None]
         for i in range(1, NBLK):
             xt_i = xin.tile([P, JT * IN], BF16, name="x_sb")
             x_sb.append(xt_i)
         wraw = const.tile([P, PARTS * 4 * D], BF16, name="wraw")
-        for g in range(PARTS):
+
+        def load_x0(g, jp):
             nc.sync.dma_start(
-                out=x0[g][:].rearrange("p (j k) -> p j k", j=JT),
-                in_=x[0:ROWS, g * D : (g + 1) * D].rearrange("(p j) k -> p j k", j=JT),
+                out=x0[g][jp][:].rearrange("p (j k) -> p j k", j=2),
+                in_=x[0:ROWS, g * D : (g + 1) * D].rearrange("(p j) k -> p j k", j=JT)[:, 2 * jp : 2 * jp + 2],
             )
+
+        def load_w(g):
             nc.sync.dma_start(
                 out=wraw[:, g * 4 * D : (g + 1) * 4 * D],
                 in_=weights[g : g + 1, :, :].rearrange("o (p t) c -> p (o t c)", t=4),
             )
+
+        load_x0(0, 0)
+        nc.sync.dma_start(out=gn_bf[0:1, 0:1], in_=gain.rearrange("(o k) -> o k", o=1))
+        nc.sync.dma_start(out=gn_bf[0:1, 16:17], in_=norm_bias.rearrange("(o k) -> o k", o=1))
+        load_x0(0, 1)
+        load_w(0)
+        load_x0(1, 0)
+        load_x0(1, 1)
+        load_w(1)
         for i in range(1, NBLK):
             nc.sync.dma_start(
                 out=x_sb[i][:],
@@ -89,7 +101,7 @@ def tile_better_transformer_t_kernel(tc, x, weights, bias, gain, norm_bias, gamm
         wc = const.tile([P, PARTS * D], U32, name="wc", align_bytes=64)
         ws = const.tile([P, PARTS * D], U8, name="ws", align_bytes=64)
 
-        xn0 = const.tile([P, JT * IN], BF16, name="xn0")
+        xn1 = const.tile([P, JT * D], BF16, name="xn1")
         late = []
         xg = {}
         xc = {}
@@ -125,16 +137,16 @@ def tile_better_transformer_t_kernel(tc, x, weights, bias, gain, norm_bias, gamm
                 in_=wgrp[:, 4 * c0 : 4 * (c0 + HC)],
             )
 
-        def norm_x(u, g, j0=0, j1=JT):
-            dst = xn0[:].rearrange("p (u j g w e) -> p u g j w e", u=2, j=JT, g=PARTS, e=2)[:, u, g, j0:j1]
-            src = x0[g][:].rearrange("p (j w u e) -> p u j w e", u=2, j=JT, e=2)[:, u, j0:j1]
+        def norm_x(u, jp):
+            dst = xn1[:].rearrange("p (u j w e) -> p u j w e", u=2, j=JT, e=2)[:, u, 2 * jp : 2 * jp + 2]
+            src = x0[1][jp][:].rearrange("p (j w u e) -> p u j w e", u=2, j=2, e=2)[:, u]
             nc.vector.tensor_scalar(
                 out=dst, in0=src, scalar1=gn[:, 0:1], scalar2=gn[:, 16:17], op0=ALU.mult, op1=ALU.add
             )
 
         def x_trans(h, jp):
             i, g = divmod(h, PARTS)
-            xw = (xn0 if i == 0 else x_sb[i])[:].bitcast(F32)
+            xw = (xn1 if h == 1 else x0[0][jp] if h == 0 else x_sb[i])[:].bitcast(F32)
             if jp == 0:
                 xg[h] = work.tile([P, 4 * ROWS], BF16, name="xg", bufs=4, align_bytes=64)
             if h < 3 and jp == 1:
@@ -144,15 +156,15 @@ def tile_better_transformer_t_kernel(tc, x, weights, bias, gain, norm_bias, gamm
             for u in range(2):
                 for jj in range(2):
                     j = 2 * jp + jj
-                    if i == 0:
-                        col = u * (JT * IN // 4) + (j * PARTS + g) * P
+                    if h == 1:
+                        col = (u * JT + j) * P
                         words = xw[:, col : col + P]
                     else:
-                        col = j * (IN // 2) + g * (D // 2)
+                        col = jj * (D // 2) if h == 0 else j * (IN // 2) + g * (D // 2)
                         words = xw[:, col + u : col + D // 2 : 2]
                     nc.tensor.transpose(xt[:, u * 256 + jj * P : u * 256 + (jj + 1) * P], words, ident[:])
             xg_h = xg[h][:, jp * 1024 : (jp + 1) * 1024]
-            if i == 0:
+            if h == 1:
                 nc.scalar.copy(
                     out=xg_h.bitcast(F32).rearrange("p (n u) -> p n u", u=2),
                     in_=xt[:].rearrange("p (u n) -> p n u", u=2),
@@ -233,7 +245,7 @@ def tile_better_transformer_t_kernel(tc, x, weights, bias, gain, norm_bias, gamm
         def x_tile(h, j):
             i, g = divmod(h, PARTS)
             if i == 0:
-                return x0[g][:, j * D : (j + 1) * D]
+                return x0[g][j // 2][:, j % 2 * D : (j % 2 + 1) * D]
             return x_sb[i][:, j * IN + g * D : j * IN + (g + 1) * D]
 
         def on_pe(h, j):
@@ -353,10 +365,9 @@ def tile_better_transformer_t_kernel(tc, x, weights, bias, gain, norm_bias, gamm
                 x_quant(h + 2)
 
         def head():
-            for jp in range(2):
-                for u in range(2):
-                    norm_x(u, 0, 2 * jp, 2 * jp + 2)
-                x_trans(0, jp)
+            x_trans(0, 0)
+            x_late()
+            x_trans(0, 1)
             w_group(0, 0, nc.vector.tensor_copy)
             params()
             w_quant(0, 0)
@@ -365,8 +376,9 @@ def tile_better_transformer_t_kernel(tc, x, weights, bias, gain, norm_bias, gamm
             x_quant(0, 0, ROWS // 2)
             x_quant(0, ROWS // 2, ROWS)
             slot(-2)
-            for u in range(2):
-                norm_x(u, 1)
+            for jp in range(2):
+                for u in range(2):
+                    norm_x(u, jp)
             w_quant(0, 1)
             x_trans(1, 0)
             x_trans(1, 1)

from contextlib import ExitStack

import concourse.mybir as mybir
from concourse.masks import make_identity

F32 = mybir.dt.float32
BF16 = mybir.dt.bfloat16
U32 = mybir.dt.uint32
U8 = mybir.dt.uint8
FP8X4 = mybir.dt.float8_e4m3fn_x4
ACT = mybir.ActivationFunctionType
ALU = mybir.AluOpType

P = 128
B = 4096
PARTS = 2
D = 512
IN = PARTS * D
ROWS = 512
JT = ROWS // P
NBLK = B // ROWS
NU = NBLK * PARTS
CC = D // P
HC = D // 2
FINE = NU - 4
FLOPS = 2 * B * D * D * PARTS


def tile_better_transformer_t_kernel(tc, x, weights, bias, gain, norm_bias, gamma, beta, out):
    nc = tc.nc
    with ExitStack() as ctx:
        const = ctx.enter_context(tc.tile_pool(name="const", bufs=1))
        xin = ctx.enter_context(tc.tile_pool(name="xin", bufs=NBLK - 1))
        work = ctx.enter_context(tc.tile_pool(name="work", bufs=3))
        psum = ctx.enter_context(tc.psum_pool(name="psum", bufs=2))

        gn_bf = const.tile([P, 32], BF16, name="gn_bf")
        nc.vector.memset(gn_bf[:], 0.0)
        ones = const.tile([P, P], BF16, name="ones")
        nc.gpsimd.memset(ones[:], 1.0)
        prm_bf = const.tile([P, P], BF16, name="prm_bf")
        nc.vector.memset(prm_bf[:], 0.0)
        nc.scalar.dma_start(out=prm_bf[0:8, :], in_=bias.rearrange("(r c) -> r c", c=P))
        nc.scalar.dma_start(out=prm_bf[8:16, :], in_=gamma.rearrange("(r c) -> r c", c=P))
        nc.scalar.dma_start(out=prm_bf[16:24, :], in_=beta.rearrange("(r c) -> r c", c=P))
        warm = const.tile([P, 1], F32, name="warm")
        nc.vector.memset(warm[:], 0.0)
        nc.scalar.activation(out=warm[:], in_=warm[:], func=ACT.Sigmoid)

        x0 = []
        for g in range(PARTS):
            x0.append([])
            for jp in range(2):
                x0_gj = const.tile([P, 2 * D], BF16, name="x0_%d%d" % (g, jp))
                x0[g].append(x0_gj)
        x_sb = [None]
        for i in range(1, NBLK):
            xt_i = xin.tile([P, JT * IN], BF16, name="x_sb")
            x_sb.append(xt_i)
        wraw = const.tile([P, PARTS * 4 * D], BF16, name="wraw")

        def load_x0(g, jp):
            nc.sync.dma_start(
                out=x0[g][jp][:].rearrange("p (j k) -> p j k", j=2),
                in_=x[0:ROWS, g * D : (g + 1) * D].rearrange("(p j) k -> p j k", j=JT)[:, 2 * jp : 2 * jp + 2],
            )

        def load_w(g):
            nc.sync.dma_start(
                out=wraw[:, g * 4 * D : (g + 1) * 4 * D],
                in_=weights[g : g + 1, :, :].rearrange("o (p t) c -> p (o t c)", t=4),
            )

        load_x0(0, 0)
        nc.sync.dma_start(out=gn_bf[0:1, 0:1], in_=gain.rearrange("(o k) -> o k", o=1))
        nc.sync.dma_start(out=gn_bf[0:1, 16:17], in_=norm_bias.rearrange("(o k) -> o k", o=1))
        load_x0(0, 1)
        load_w(0)
        load_x0(1, 0)
        load_x0(1, 1)
        load_w(1)
        for i in range(1, NBLK):
            nc.sync.dma_start(
                out=x_sb[i][:],
                in_=x[i * ROWS : (i + 1) * ROWS, :].rearrange("(p j) k -> p (j k)", j=JT),
            )

        ident = const.tile([P, P], F32, name="ident")
        make_identity(nc, ident[:])
        ident_bf = const.tile([P, P], BF16, name="ident_bf")
        nc.vector.tensor_copy(out=ident_bf[:], in_=ident[:])

        gn = const.tile([P, 32], F32, name="gn")
        gn_ps = psum.tile([P, 32], F32, name="gn_ps", tag="ot")
        nc.tensor.matmul(gn_ps[:], lhsT=ones[:], rhs=gn_bf[:], start=True, stop=True)
        nc.vector.tensor_copy(out=gn[:], in_=gn_ps[:])
        prm = const.tile([P, 32], F32, name="prm")
        bb = const.tile([P, 8], F32, name="bb")
        dd = const.tile([P, 8], F32, name="dd")
        wgrp = const.tile([P, PARTS * 4 * D], BF16, name="wgrp", align_bytes=64)
        wc = const.tile([P, PARTS * D], U32, name="wc", align_bytes=64)
        ws = const.tile([P, PARTS * D], U8, name="ws", align_bytes=64)

        xn1 = const.tile([P, JT * D], BF16, name="xn1")
        late = []
        xg = {}
        xc = {}
        xs = {}
        acc = {}
        sg = {}
        mm = {}
        op = {}
        ob = {}
        ots = {}

        def params():
            prm_ps = psum.tile([P, P], BF16, name="prm_ps", tag="ot")
            nc.tensor.transpose(prm_ps[:], prm_bf[:], ident_bf[:])
            nc.vector.tensor_copy(out=prm[:], in_=prm_ps[:, 0:32])

        def params2():
            nc.vector.tensor_tensor(out=bb[:], in0=prm[:, 16:24], in1=prm[:, 0:8], op=ALU.mult)
            nc.vector.tensor_scalar(out=dd[:], in0=prm[:, 8:16], scalar1=-1.0, scalar2=1.0, op0=ALU.mult, op1=ALU.add)

        def w_group(g, hf, copy):
            lo = hf * HC
            copy(
                out=wgrp[:].rearrange("p (g c t) -> p g c t", g=PARTS, t=4)[:, g, lo : lo + HC, :],
                in_=wraw[:].rearrange("p (g t c) -> p g c t", g=PARTS, t=4)[:, g, lo : lo + HC, :],
            )

        def w_quant(g, hf):
            c0 = g * D + hf * HC
            nc.vector.quantize_mx(
                out=wc[:, c0 : c0 + HC].bitcast(FP8X4),
                scales=ws[:, c0 : c0 + HC],
                in_=wgrp[:, 4 * c0 : 4 * (c0 + HC)],
            )

        def norm_x(u, jp):
            dst = xn1[:].rearrange("p (u j w e) -> p u j w e", u=2, j=JT, e=2)[:, u, 2 * jp : 2 * jp + 2]
            src = x0[1][jp][:].rearrange("p (j w u e) -> p u j w e", u=2, j=2, e=2)[:, u]
            nc.vector.tensor_scalar(
                out=dst, in0=src, scalar1=gn[:, 0:1], scalar2=gn[:, 16:17], op0=ALU.mult, op1=ALU.add
            )

        def x_trans(h, jp):
            i, g = divmod(h, PARTS)
            xw = (xn1 if h == 1 else x0[0][jp] if h == 0 else x_sb[i])[:].bitcast(F32)
            if jp == 0:
                xg[h] = work.tile([P, 4 * ROWS], BF16, name="xg", bufs=4, align_bytes=64)
            if h < 3 and jp == 1:
                xt = psum.tile([P, 512], F32, name="xt", tag="ot")
            else:
                xt = psum.tile([P, 512], F32, name="xt", tag="xt", bufs=1)
            for u in range(2):
                for jj in range(2):
                    j = 2 * jp + jj
                    if h == 1:
                        col = (u * JT + j) * P
                        words = xw[:, col : col + P]
                    else:
                        col = jj * (D // 2) if h == 0 else j * (IN // 2) + g * (D // 2)
                        words = xw[:, col + u : col + D // 2 : 2]
                    nc.tensor.transpose(xt[:, u * 256 + jj * P : u * 256 + (jj + 1) * P], words, ident[:])
            xg_h = xg[h][:, jp * 1024 : (jp + 1) * 1024]
            if h == 1:
                nc.scalar.copy(
                    out=xg_h.bitcast(F32).rearrange("p (n u) -> p n u", u=2),
                    in_=xt[:].rearrange("p (u n) -> p n u", u=2),
                )
                return
            dst = xg_h.rearrange("p (n u e) -> p n u e", u=2, e=2)
            src = xt[:].bitcast(BF16).rearrange("p (u n e) -> p n u e", u=2, e=2)
            if jp == 0:
                late.append((dst, src))
            else:
                nc.scalar.activation(out=dst, in_=src, func=ACT.Identity, scale=gn[:, 0:1], bias=gn[:, 16:17])

        def x_late():
            while late:
                dst, src = late.pop(0)
                nc.vector.tensor_scalar(
                    out=dst, in0=src, scalar1=gn[:, 0:1], scalar2=gn[:, 16:17], op0=ALU.mult, op1=ALU.add
                )

        def x_quant(h, lo=0, hi=ROWS):
            if lo == 0:
                xc[h] = work.tile([P, ROWS], U32, name="xc", align_bytes=64)
                xs[h] = work.tile([P, ROWS], U8, name="xs", align_bytes=64)
            nc.vector.quantize_mx(
                out=xc[h][:, lo:hi].bitcast(FP8X4), scales=xs[h][:, lo:hi], in_=xg[h][:, 4 * lo : 4 * hi]
            )

        def mx(h, k):
            q = (h % PARTS) * CC + k
            a = psum.tile([P, ROWS], F32, name="acc", tag="acc", bufs=5)
            acc[(h, k)] = a
            nc.tensor.matmul_mx(
                out=a[:],
                lhsT=wc[:, q * P : (q + 1) * P].bitcast(FP8X4),
                lhsT_scale=ws[:, q * P : (q + 1) * P],
                rhs=xc[h][:].bitcast(FP8X4),
                rhs_scale=xs[h][:],
                start=True,
                stop=True,
            )

        def sig(h, k):
            q = (h % PARTS) * CC + k
            s = work.tile([P, ROWS], F32, name="sg", bufs=5)
            nc.scalar.activation(
                out=s[:], in_=acc[(h, k)][:], func=ACT.Sigmoid, scale=prm[:, 16 + q : 17 + q], bias=bb[:, q : q + 1]
            )
            sg[(h, k)] = s
            if h > 0:
                mult(h, k, nc.gpsimd)

        def mult(h, k, eng):
            q = (h % PARTS) * CC + k
            m = work.tile([P, ROWS], F32, name="mm", bufs=8)
            mm[(h, k)] = m
            eng.tensor_scalar(
                out=m[:],
                in0=sg[(h, k)][:],
                scalar1=dd[:, q : q + 1],
                scalar2=prm[:, 8 + q : 9 + q],
                op0=ALU.mult,
                op1=ALU.add,
            )

        def prod(h, k, lo=0, hi=ROWS):
            q = (h % PARTS) * CC + k
            if k == 0:
                op[h] = work.tile([P, CC * ROWS], F32, name="op", bufs=4)
            nc.vector.scalar_tensor_tensor(
                out=op[h][:, k * ROWS + lo : k * ROWS + hi],
                in0=acc[(h, k)][:, lo:hi],
                scalar=prm[:, q : q + 1],
                in1=mm[(h, k)][:, lo:hi],
                op0=ALU.add,
                op1=ALU.mult,
            )

        def x_tile(h, j):
            i, g = divmod(h, PARTS)
            if i == 0:
                return x0[g][j // 2][:, j % 2 * D : (j % 2 + 1) * D]
            return x_sb[i][:, j * IN + g * D : j * IN + (g + 1) * D]

        def on_pe(h, j):
            return j == 1 or (j == 3 and (h % 2 == 1 or h == NU - 2))

        def on_gpsimd(h, j):
            return j == 3 and h % 2 == 0 and 2 <= h <= 12

        def back(h, j, ks=range(CC), tag="ot"):
            if ks[0] == 0:
                ot = psum.tile([P, D], F32, name="ot", tag=tag, bufs=5 if tag == "acc" else 2)
                ots[(h, j)] = ot
            ot = ots[(h, j)]
            if on_pe(h, j) and ks[0] == 0:
                nc.tensor.matmul(
                    ot[:], lhsT=ident_bf[:], rhs=x_tile(h, j), start=True, stop=False
                )
            for k in ks:
                nc.tensor.matmul(
                    ot[:, k * P : (k + 1) * P],
                    lhsT=op[h][:, k * ROWS + j * P : k * ROWS + (j + 1) * P],
                    rhs=ident[:],
                    is_transpose=True,
                    start=not on_pe(h, j),
                    stop=not on_pe(h, j) or k == CC - 1,
                )
            if (on_pe(h, j) or on_gpsimd(h, j)) and ks[-1] == CC - 1:
                finish(h, j)

        def finish(h, j):
            if h not in ob:
                ob[h] = work.tile([P, JT * D], F32, name="ob", bufs=7)
            dst = ob[h][:, j * D : (j + 1) * D]
            if on_pe(h, j) or on_gpsimd(h, j):
                nc.scalar.copy(out=dst, in_=ots[(h, j)][:])
                if on_gpsimd(h, j):
                    nc.gpsimd.tensor_tensor(out=dst, in0=dst, in1=x_tile(h, j), op=ALU.add)
            else:
                nc.vector.tensor_tensor(
                    out=dst,
                    in0=x_tile(h, j),
                    in1=ots[(h, j)][:],
                    op=ALU.add,
                )

        def store(h, j0, j1):
            i, g = divmod(h, PARTS)
            dst = out[i * ROWS : (i + 1) * ROWS, g * D : (g + 1) * D].rearrange("(p j) c -> p j c", j=JT)
            src = ob[h][:].rearrange("p (j c) -> p j c", j=JT)
            nc.sync.dma_start(out=dst[:, j0:j1, :], in_=src[:, j0:j1, :])

        def ok(h):
            return 0 <= h < NU

        def trans_at(n):
            if n < 0:
                return []
            if n == 0:
                return [4, 5]
            return [n + 5]

        def slot(n):
            h, b = divmod(n, 2)
            last = h == NU - 1 and b == 1
            if ok(h):
                if h == 0:
                    mult(h, 2 * b, nc.vector)
                    mult(h, 2 * b + 1, nc.vector)
                prod(h, 2 * b)
                if n == 0:
                    w_quant(1, 0)
                    x_quant(1)
                    w_quant(1, 1)
                if n == 2:
                    x_quant(2)
                x_late()
                if ok(h - 1) and not last:
                    finish(h - 1, 2 * b)
                    if b == 0 and h > FINE:
                        store(h - 1, 0, 2)
                if not last:
                    prod(h, 2 * b + 1)
            if last:
                prod(h, CC - 1, 0, ROWS // 2)
                prod(h, CC - 1, ROWS // 2, ROWS)
                store(h - 1, 3, JT)
                finish(h - 1, 2)
                store(h - 1, 2, 3)
                for j in range(JT - 1):
                    back(h, j, range(CC - 1), "acc")
                for j in range(JT - 1):
                    back(h, j, [CC - 1])
                back(h, JT - 1)
                for j in range(JT):
                    if not on_pe(h, j):
                        finish(h, j)
                    store(h, j, j + 1)
            if ok(h + 1):
                mx(h + 1, 2 * b)
                mx(h + 1, 2 * b + 1)
                sig(h + 1, 2 * b)
                sig(h + 1, 2 * b + 1)
            if b == 1 and ok(h - 1) and not last:
                if not on_pe(h - 1, 3) and not on_gpsimd(h - 1, 3):
                    finish(h - 1, 3)
                store(h - 1, 2 if h > FINE else 0, JT)
            for m in trans_at(n):
                if ok(m // 2):
                    x_trans(m // 2, m % 2)
            if b == 1 and ok(h) and not last:
                back(h, 0)
                back(h, 1)
            if b == 0 and ok(h - 1):
                back(h - 1, 2)
                back(h - 1, 3)
            if b == 1 and ok(h + 2) and h > 0:
                x_quant(h + 2)

        def head():
            x_trans(0, 0)
            x_late()
            x_trans(0, 1)
            w_group(0, 0, nc.vector.tensor_copy)
            params()
            w_quant(0, 0)
            w_group(0, 1, nc.scalar.copy)
            params2()
            x_quant(0, 0, ROWS // 2)
            x_quant(0, ROWS // 2, ROWS)
            slot(-2)
            for jp in range(2):
                for u in range(2):
                    norm_x(u, jp)
            w_quant(0, 1)
            x_trans(1, 0)
            x_trans(1, 1)
            w_group(1, 0, nc.vector.tensor_copy)
            w_group(1, 1, nc.vector.tensor_copy)
            slot(-1)

        def main():
            head()
            for n in range(2 * NU):
                slot(n)

        with tc.manual_schedule():
            main()
